import numpy as np
import ml_dtypes


def mxq(x, axis, fmt="e4m3"):
    dtype, down = {"e4m3": (ml_dtypes.float8_e4m3fn, 7), "e5m2": (ml_dtypes.float8_e5m2, 14)}[fmt]
    v = np.moveaxis(np.asarray(x, np.float32).astype(ml_dtypes.bfloat16).astype(np.float64), axis, -1)
    blocks = v.reshape(v.shape[:-1] + (-1, 32))
    amax = np.abs(blocks).max(-1, keepdims=True)
    byte = np.maximum(np.where(amax > 0, np.frexp(amax)[1] - 1 + 127, 0) - down, 1)
    scale = np.exp2(byte - 127.0)
    codes = (blocks / scale).astype(np.float32).astype(dtype).astype(np.float64)
    return np.moveaxis((codes * scale).reshape(v.shape), -1, axis)


WIDE = False


def mx_kscale(k):
    if not WIDE:
        return np.ones(k)
    levels = np.array([10, -10, 5, -5, 0])
    a = np.random.permutation(np.resize(levels, k // 512 * 4)).reshape(k // 512, 4)
    idx = np.arange(k)
    return np.exp2(a[idx // 512, idx % 128 // 32])


BF16 = ml_dtypes.bfloat16


def bf(x):
    return np.asarray(x, np.float32).astype(BF16)


def f64(x):
    return np.asarray(x).astype(np.float64)


E2M1 = np.array([0.0, 0.5, 1.0, 1.5, 2.0, 3.0, 4.0, 6.0, -0.0, -0.5, -1.0, -1.5, -2.0, -3.0, -4.0, -6.0])


def pack_weight(w, fmt):
    k, n = w.shape
    w = f64(bf(w)).reshape(k // 32, 32, n)
    amax = np.abs(w).max(1)
    if fmt == "e4m3":
        byte = np.frexp(amax)[1] - 1 + 127 - 7
    else:
        mant, ex = np.frexp(amax / 6.0)
        byte = np.where(mant > 0.5, ex, ex - 1) + 127
    byte = np.clip(np.where(amax > 0, byte, 1), 1, 254)
    scaled = (w * np.exp2(127.0 - byte)[:, None, :]).reshape(k, n).astype(np.float32)
    by_word = np.ascontiguousarray(scaled.reshape(k // 512, 128, 4, n).transpose(0, 1, 3, 2))
    if fmt == "e4m3":
        words = by_word.astype(ml_dtypes.float8_e4m3fn).view(np.uint8)
    else:
        c = by_word.astype(ml_dtypes.float4_e2m1fn).view(np.uint8) & 0xF
        words = c[..., 0::2] | (c[..., 1::2] << 4)
    return np.ascontiguousarray(words), np.ascontiguousarray(byte.astype(np.uint8).reshape(k // 512, 16, n))


def unpack_weight(words, scales, fmt):
    g, p, n, _ = words.shape
    if fmt == "e4m3":
        vals = np.ascontiguousarray(words).view(ml_dtypes.float8_e4m3fn).astype(np.float64)
    else:
        nib = np.empty((g, p, n, 4), np.uint8)
        nib[..., 0::2] = words & 0xF
        nib[..., 1::2] = words >> 4
        vals = E2M1[nib]
    vals = vals * np.repeat(np.exp2(scales.astype(np.float64) - 127.0), 8, axis=1)[..., None]
    return vals.transpose(0, 1, 3, 2).reshape(g * 512, n)


B, C_IN, C_OUT, N, T, K = 1, 512, 128, 1024, 3, 3
FMT = 'e4m3'


def cheb_laplacian(p):
    adj = 1.0 / (1.0 + np.exp(-p))
    adj = (adj + adj.T) * 0.5
    adj = adj * (1.0 - np.eye(N))
    deg = adj.sum(axis=1)
    dis = 1.0 / np.sqrt(deg)
    return -(dis[:, None] * adj * dis[None, :])


def setup_inputs():
    s = mx_kscale(C_IN)
    x = np.random.standard_normal((B, C_IN, 1, T)) + np.random.standard_normal((B, C_IN, N, T))
    adj_param = bf(4.0 * np.random.standard_normal((N, N)) - 10.0 + 10.0 * np.eye(N))
    w_cheb0_words, w_cheb0_scales = pack_weight(np.random.standard_normal((C_IN, C_OUT)) / np.sqrt(C_IN) / s[:, None], FMT)
    w_cheb1_words, w_cheb1_scales = pack_weight(np.random.standard_normal((C_IN, C_OUT)) / np.sqrt(C_IN) / s[:, None], FMT)
    return {'x': bf(x * s[None, :, None, None]),
            'adj_param': adj_param,
            'w_cheb0_words': w_cheb0_words,
            'w_cheb0_scales': w_cheb0_scales,
            'w_cheb1_words': w_cheb1_words,
            'w_cheb1_scales': w_cheb1_scales}


def reference(x, adj_param, w_cheb0_words, w_cheb0_scales, w_cheb1_words, w_cheb1_scales):
    s = cheb_laplacian(f64(adj_param))
    xt = f64(x).transpose(0, 3, 2, 1)
    h = mxq(xt, 3, 'e4m3') @ unpack_weight(w_cheb0_words, w_cheb0_scales, FMT)
    tx1 = mxq(s, 1, 'e4m3') @ mxq(xt, 2, 'e4m3')
    h = h + (mxq(tx1, 3, 'e4m3') @ unpack_weight(w_cheb1_words, w_cheb1_scales, FMT))
    return h

@@ -1,0 +1,302 @@
+import concourse.mybir as mybir
+from concourse.masks import make_identity
+
+F32 = mybir.dt.float32
+BF16 = mybir.dt.bfloat16
+U32 = mybir.dt.uint32
+U8 = mybir.dt.uint8
+I32 = mybir.dt.int32
+FP8X4 = mybir.dt.float8_e4m3fn_x4
+ACT = mybir.ActivationFunctionType
+ALU = mybir.AluOpType
+AXIS = mybir.AxisListType
+
+P = 128
+PACK = 4
+NODES = 1024
+CHANNELS = 512
+TIMES = 3
+OUTS = 128
+CHUNKS = NODES // P
+PASSES = NODES // (P * PACK)
+BANK = 512
+HALVES = NODES // BANK
+PIECES = 4
+PIECE_NODES = NODES // PIECES
+QUARTER = NODES // PACK
+SLICE = P // PACK
+
+FLOPS = 2 * TIMES * NODES * (NODES * CHANNELS + 2 * CHANNELS * OUTS)
+
+
+def tile_dynamicgraphspatialconv_pa_kernel(
+    tc, x, adj_param, w_cheb0_words, w_cheb0_scales, w_cheb1_words, w_cheb1_scales, out
+):
+    nc = tc.nc
+    with (
+        tc.tile_pool(name="keep", bufs=1) as keep,
+        tc.tile_pool(name="adj_in", bufs=4) as adj_in,
+        tc.tile_pool(name="x_in", bufs=2) as x_in,
+        tc.tile_pool(name="stage", bufs=3) as stage,
+        tc.psum_pool(name="banks", bufs=4) as banks,
+        tc.psum_pool(name="row_banks", bufs=1) as row_banks,
+        tc.psum_pool(name="out_banks", bufs=2) as out_banks,
+    ):
+        ident = keep.tile([P, P], F32)
+        make_identity(nc, ident[:])
+        ident_bf = keep.tile([P, P], BF16)
+        make_identity(nc, ident_bf[:])
+
+        weights = []
+        for name, words_in, scales_in in (
+            ("w0", w_cheb0_words, w_cheb0_scales),
+            ("w1", w_cheb1_words, w_cheb1_scales),
+        ):
+            words = keep.tile([P, OUTS], U32, name=name + "_words", align_bytes=64)
+            plane = keep.tile([P, OUTS], U8, name=name + "_plane", align_bytes=64)
+            nc.vector.memset(plane[:].bitcast(I32), 0)
+            weights.append((words, plane, words_in, scales_in))
+
+        x_rows = x[0].rearrange("(p j) n t -> p j (n t)", j=PACK)
+        adj_tiles = []
+        x_tiles = []
+
+        def load_adj(r):
+            adj_sb = adj_in.tile([P, NODES], BF16, name="adj_sb")
+            nc.sync.dma_start(out=adj_sb[:], in_=adj_param[r * P : (r + 1) * P, :])
+            adj_tiles.append(adj_sb)
+
+        def load_x(i):
+            width = PIECE_NODES * TIMES
+            x_sb = x_in.tile([P, PACK, width], BF16, name="x_sb")
+            nc.sync.dma_start(out=x_sb[:], in_=x_rows[:, :, i * width : (i + 1) * width])
+            x_tiles.append(x_sb)
+
+        x_quarters = x[0].rearrange("c (jn n) t -> c jn (n t)", jn=PACK)
+        x_sliced = keep.tile([P, PACK, PACK, QUARTER * TIMES], BF16)
+
+        def load_x_slice(j, k):
+            nc.sync.dma_start(
+                out=x_sliced[:, j, k, :], in_=x_quarters[k * P + j : (k + 1) * P : PACK, :, :]
+            )
+
+        sig = keep.tile([P, CHUNKS, NODES], F32)
+
+        def sigmoid_chunk(r):
+            nc.scalar.activation(out=sig[:, r, :], in_=adj_tiles[r][:], func=ACT.Sigmoid)
+            diag = sig[:, r, r * P : (r + 1) * P]
+            nc.gpsimd.affine_select(
+                out=diag,
+                in_=diag,
+                pattern=[[-1, P]],
+                compare_op=ALU.not_equal,
+                fill=0.0,
+                base=0,
+                channel_multiplier=1,
+            )
+
+        x_by_c = keep.tile([P, TIMES, NODES, PACK], BF16, align_bytes=64)
+        xc_words = keep.tile([P, TIMES, NODES], U32, align_bytes=64)
+        xc_plane = keep.tile([P, TIMES, NODES], U8, align_bytes=64)
+
+        def group_channels(i):
+            nodes = slice(i * PIECE_NODES, (i + 1) * PIECE_NODES)
+            src = x_tiles[i][:].rearrange("p j (n t) -> p t n j", t=TIMES)
+            for t in range(TIMES):
+                nc.gpsimd.tensor_scalar(
+                    out=x_by_c[:, t, nodes, :], in0=src[:, t], scalar1=1.0, scalar2=0.0,
+                    op0=ALU.mult, op1=ALU.add,
+                )
+            for t in range(TIMES):
+                nc.vector.quantize_mx(
+                    out=xc_words[:, t, nodes].bitcast(FP8X4),
+                    scales=xc_plane[:, t, nodes],
+                    in_=x_by_c[:, t, nodes, :].rearrange("p n j -> p (n j)"),
+                )
+
+        slices = [(j, k) for j in range(PACK) for k in range(PACK)]
+        for r in range(CHUNKS):
+            load_adj(r)
+            load_x_slice(*slices[r])
+        for j, k in slices[CHUNKS:]:
+            load_x_slice(j, k)
+        for i in range(PIECES):
+            load_x(i)
+        for words, plane, words_in, scales_in in weights:
+            nc.sync.dma_start(
+                out=words[:].bitcast(I32),
+                in_=words_in[0].rearrange("p n t -> p (n t)").bitcast(I32),
+            )
+            for q in range(4):
+                nc.sync.dma_start(
+                    out=plane[32 * q : 32 * q + 4, :].bitcast(I32),
+                    in_=scales_in[0, 4 * q : 4 * q + 4, :].bitcast(I32),
+                )
+
+        for r in range(CHUNKS):
+            sigmoid_chunk(r)
+        warm = keep.tile([P, 1], F32)
+        nc.scalar.activation(out=warm[:], in_=sig[:, CHUNKS - 1, 0:1], func=ACT.Sqrt)
+
+        a2 = keep.tile([P, CHUNKS, NODES], F32)
+        deg_parts = keep.tile([P, CHUNKS, HALVES], F32)
+        for h in range(HALVES):
+            for r in range(CHUNKS):
+                sig_t = banks.tile([P, BANK], F32, name="bank")
+                for i in range(BANK // P):
+                    nc.tensor.transpose(
+                        sig_t[:, i * P : (i + 1) * P],
+                        sig[:, h * (BANK // P) + i, r * P : (r + 1) * P],
+                        ident[:],
+                    )
+                cols = slice(h * BANK, (h + 1) * BANK)
+                nc.vector.scalar_tensor_tensor(
+                    out=a2[:, r, cols], in0=sig[:, r, cols], scalar=1.0, in1=sig_t[:],
+                    op0=ALU.mult, op1=ALU.add, accum_out=deg_parts[:, r, h : h + 1],
+                )
+
+        xn_words = keep.tile([P, TIMES, PASSES, CHANNELS], U32, align_bytes=64)
+        xn_plane = keep.tile([P, TIMES, PASSES, CHANNELS], U8, align_bytes=64)
+        x_by_time = x_sliced[:].rearrange("p j k (n t) -> p j k t n", t=TIMES)
+        x_by_n = {}
+        for g in range(PASSES):
+            for t in range(TIMES):
+                x_by_n[g, t] = keep.tile(
+                    [P, PACK, P * PACK], BF16, name="x_by_n_%d_%d" % (g, t), align_bytes=64
+                )
+        for j in range(PACK):
+            for g in range(PASSES):
+                for t in range(TIMES):
+                    x_t = banks.tile([P, BANK], BF16, name="bank")
+                    for k in range(PACK):
+                        nc.tensor.transpose(
+                            x_t[:, k * P : (k + 1) * P],
+                            x_by_time[:, j, k, t, g * P : (g + 1) * P],
+                            ident_bf[:],
+                        )
+                    nc.scalar.copy(out=x_by_n[g, t][:, j, :], in_=x_t[:])
+        for g in range(PASSES):
+            for t in range(TIMES):
+                nc.vector.quantize_mx(
+                    out=xn_words[:, t, g, :].bitcast(FP8X4),
+                    scales=xn_plane[:, t, g, :],
+                    in_=x_by_n[g, t][:].rearrange("p j c -> p (j c)"),
+                )
+
+        deg = keep.tile([P, CHUNKS], F32)
+        nc.vector.tensor_reduce(out=deg[:], in_=deg_parts[:], axis=AXIS.X, op=ALU.add)
+        root = keep.tile([P, CHUNKS], F32)
+        nc.scalar.activation(out=root[:], in_=deg[:], func=ACT.Sqrt)
+        r_col = keep.tile([P, CHUNKS], F32)
+        nc.vector.reciprocal(out=r_col[:], in_=root[:])
+        neg_r_col = keep.tile([P, CHUNKS], F32)
+        nc.vector.tensor_scalar(
+            out=neg_r_col[:], in0=r_col[:], scalar1=-1.0, scalar2=None, op0=ALU.mult
+        )
+        r_rep = keep.tile([P, CHUNKS, P], F32)
+        nc.vector.tensor_copy(out=r_rep[:], in_=r_col[:].unsqueeze(2).to_broadcast([P, CHUNKS, P]))
+        r_rows = []
+        for h in range(HALVES):
+            r_row = row_banks.tile([P, BANK], F32, name="r_row%d" % h)
+            for i in range(BANK // P):
+                nc.tensor.transpose(r_row[:, i * P : (i + 1) * P], r_rep[:, h * (BANK // P) + i, :], ident[:])
+            r_rows.append(r_row)
+
+        def scale_rows(h):
+            cols = slice(h * BANK, (h + 1) * BANK)
+            for r in range(CHUNKS):
+                if r % 3 == 0:
+                    nc.scalar.activation(
+                        out=a2[:, r, cols], in_=a2[:, r, cols], func=ACT.Copy,
+                        scale=neg_r_col[:, r : r + 1],
+                    )
+                else:
+                    nc.vector.tensor_scalar(
+                        out=a2[:, r, cols], in0=a2[:, r, cols], scalar1=neg_r_col[:, r : r + 1],
+                        scalar2=None, op0=ALU.mult,
+                    )
+
+        s_words = keep.tile([P, CHUNKS, PASSES * P], U32, align_bytes=64)
+        s_plane = keep.tile([P, CHUNKS, PASSES * P], U8, align_bytes=64)
+        tx_tiles = {}
+
+        def graph_columns(v):
+            cols = slice(v * P, (v + 1) * P)
+            s_by_n = stage.tile([P, PASSES, P, PACK], BF16, name="s_by_n", align_bytes=64)
+            row = r_rows[v // (BANK // P)][:, (v % (BANK // P)) * P : (v % (BANK // P) + 1) * P]
+            nc.vector.tensor_tensor(
+                out=s_by_n[:],
+                in0=a2[:, :, cols].rearrange("p (jn g) q -> p g q jn", g=PASSES),
+                in1=row.unsqueeze(1).unsqueeze(3).to_broadcast([P, PASSES, P, PACK]),
+                op=ALU.mult,
+            )
+            nc.vector.quantize_mx(
+                out=s_words[:, v, :].bitcast(FP8X4),
+                scales=s_plane[:, v, :],
+                in_=s_by_n[:].rearrange("p g q jn -> p (g q jn)"),
+            )
+
+        def node_matmul(v):
+            tx_by_c = stage.tile([P, TIMES, P * PACK], BF16, name="tx_by_c", align_bytes=64)
+            tx_words = stage.tile([P, TIMES, P], U32, name="tx_words", align_bytes=64)
+            tx_plane = stage.tile([P, TIMES, P], U8, name="tx_plane", align_bytes=64)
+            for t in range(TIMES):
+                tx = banks.tile([P, BANK], F32, name="bank")
+                for j in range(PACK):
+                    for g in range(PASSES):
+                        nc.tensor.matmul_mx(
+                            out=tx[:, j * P : (j + 1) * P],
+                            lhsT=xn_words[:, t, g, j * P : (j + 1) * P].bitcast(FP8X4),
+                            lhsT_scale=xn_plane[:, t, g, j * P : (j + 1) * P],
+                            rhs=s_words[:, v, g * P : (g + 1) * P].bitcast(FP8X4),
+                            rhs_scale=s_plane[:, v, g * P : (g + 1) * P],
+                            start=(g == 0),
+                            stop=(g == PASSES - 1),
+                        )
+                dst = tx_by_c[:, t, :].rearrange("p (q j) -> p q j", j=PACK)
+                src = tx[:].rearrange("p (j q) -> p q j", j=PACK)
+                nc.scalar.copy(out=dst, in_=src)
+            for t in range(TIMES):
+                nc.vector.quantize_mx(
+                    out=tx_words[:, t, :].bitcast(FP8X4), scales=tx_plane[:, t, :], in_=tx_by_c[:, t, :]
+                )
+            tx_tiles[v] = (tx_words, tx_plane)
+
+        def channel_matmuls(v):
+            tx_words, tx_plane = tx_tiles[v]
+            acc = out_banks.tile([P, TIMES, OUTS], F32, name="acc")
+            for t in range(TIMES):
+                nc.tensor.matmul_mx(
+                    out=acc[:, t, :],
+                    lhsT=xc_words[:, t, v * P : (v + 1) * P].bitcast(FP8X4),
+                    lhsT_scale=xc_plane[:, t, v * P : (v + 1) * P],
+                    rhs=weights[0][0][:].bitcast(FP8X4),
+                    rhs_scale=weights[0][1][:],
+                    start=True,
+                    stop=False,
+                )
+                nc.tensor.matmul_mx(
+                    out=acc[:, t, :],
+                    lhsT=tx_words[:, t, :].bitcast(FP8X4),
+                    lhsT_scale=tx_plane[:, t, :],
+                    rhs=weights[1][0][:].bitcast(FP8X4),
+                    rhs_scale=weights[1][1][:],
+                    start=False,
+                    stop=True,
+                )
+            result = stage.tile([P, TIMES, OUTS], F32, name="result")
+            nc.scalar.copy(out=result[:], in_=acc[:])
+            nc.sync.dma_start(
+                out=out[0, :, v * P : (v + 1) * P, :].rearrange("t q o -> q t o"), in_=result[:]
+            )
+
+        for v in range(CHUNKS):
+            if v % (BANK // P) == 0:
+                scale_rows(v // (BANK // P))
+            if v % 2 == 0:
+                group_channels(v // 2)
+            graph_columns(v)
+            node_matmul(v)
+            if v > 0:
+                channel_matmuls(v - 1)
+        channel_matmuls(CHUNKS - 1)

@@ -23,8 +23,6 @@ BANK = 512
 HALVES = NODES // BANK
 PIECES = 4
 PIECE_NODES = NODES // PIECES
-QUARTER = NODES // PACK
-SLICE = P // PACK
 
 FLOPS = 2 * TIMES * NODES * (NODES * CHANNELS + 2 * CHANNELS * OUTS)
 
@@ -36,7 +34,7 @@ def tile_dynamicgraphspatialconv_pa_kernel(
     with (
         tc.tile_pool(name="keep", bufs=1) as keep,
         tc.tile_pool(name="adj_in", bufs=4) as adj_in,
-        tc.tile_pool(name="x_in", bufs=2) as x_in,
+        tc.tile_pool(name="x_in", bufs=PIECES) as x_in,
         tc.tile_pool(name="stage", bufs=3) as stage,
         tc.psum_pool(name="banks", bufs=4) as banks,
         tc.psum_pool(name="row_banks", bufs=1) as row_banks,
@@ -44,8 +42,6 @@ def tile_dynamicgraphspatialconv_pa_kernel(
     ):
         ident = keep.tile([P, P], F32)
         make_identity(nc, ident[:])
-        ident_bf = keep.tile([P, P], BF16)
-        make_identity(nc, ident_bf[:])
 
         weights = []
         for name, words_in, scales_in in (
@@ -72,14 +68,6 @@ def tile_dynamicgraphspatialconv_pa_kernel(
             nc.sync.dma_start(out=x_sb[:], in_=x_rows[:, :, i * width : (i + 1) * width])
             x_tiles.append(x_sb)
 
-        x_quarters = x[0].rearrange("c (jn n) t -> c jn (n t)", jn=PACK)
-        x_sliced = keep.tile([P, PACK, PACK, QUARTER * TIMES], BF16)
-
-        def load_x_slice(j, k):
-            nc.sync.dma_start(
-                out=x_sliced[:, j, k, :], in_=x_quarters[k * P + j : (k + 1) * P : PACK, :, :]
-            )
-
         sig = keep.tile([P, CHUNKS, NODES], F32)
 
         def sigmoid_chunk(r):
@@ -96,32 +84,21 @@ def tile_dynamicgraphspatialconv_pa_kernel(
             )
 
         x_by_c = keep.tile([P, TIMES, NODES, PACK], BF16, align_bytes=64)
-        xc_words = keep.tile([P, TIMES, NODES], U32, align_bytes=64)
-        xc_plane = keep.tile([P, TIMES, NODES], U8, align_bytes=64)
 
         def group_channels(i):
             nodes = slice(i * PIECE_NODES, (i + 1) * PIECE_NODES)
             src = x_tiles[i][:].rearrange("p j (n t) -> p t n j", t=TIMES)
-            for t in range(TIMES):
+            nc.vector.tensor_copy(out=x_by_c[:, 0, nodes, :], in_=src[:, 0])
+            for t in range(1, TIMES):
                 nc.gpsimd.tensor_scalar(
                     out=x_by_c[:, t, nodes, :], in0=src[:, t], scalar1=1.0, scalar2=0.0,
                     op0=ALU.mult, op1=ALU.add,
                 )
-            for t in range(TIMES):
-                nc.vector.quantize_mx(
-                    out=xc_words[:, t, nodes].bitcast(FP8X4),
-                    scales=xc_plane[:, t, nodes],
-                    in_=x_by_c[:, t, nodes, :].rearrange("p n j -> p (n j)"),
-                )
 
-        slices = [(j, k) for j in range(PACK) for k in range(PACK)]
         for r in range(CHUNKS):
             load_adj(r)
-            load_x_slice(*slices[r])
-        for j, k in slices[CHUNKS:]:
-            load_x_slice(j, k)
-        for i in range(PIECES):
-            load_x(i)
+            if r % 2 == 1:
+                load_x(r // 2)
         for words, plane, words_in, scales_in in weights:
             nc.sync.dma_start(
                 out=words[:].bitcast(I32),
@@ -135,6 +112,8 @@ def tile_dynamicgraphspatialconv_pa_kernel(
 
         for r in range(CHUNKS):
             sigmoid_chunk(r)
+            if r % 2 == 1:
+                group_channels(r // 2)
         warm = keep.tile([P, 1], F32)
         nc.scalar.activation(out=warm[:], in_=sig[:, CHUNKS - 1, 0:1], func=ACT.Sqrt)
 
@@ -155,33 +134,37 @@ def tile_dynamicgraphspatialconv_pa_kernel(
                     op0=ALU.mult, op1=ALU.add, accum_out=deg_parts[:, r, h : h + 1],
                 )
 
+        x_words = x_by_c[:].bitcast(F32)
         xn_words = keep.tile([P, TIMES, PASSES, CHANNELS], U32, align_bytes=64)
         xn_plane = keep.tile([P, TIMES, PASSES, CHANNELS], U8, align_bytes=64)
-        x_by_time = x_sliced[:].rearrange("p j k (n t) -> p j k t n", t=TIMES)
-        x_by_n = {}
         for g in range(PASSES):
             for t in range(TIMES):
-                x_by_n[g, t] = keep.tile(
-                    [P, PACK, P * PACK], BF16, name="x_by_n_%d_%d" % (g, t), align_bytes=64
-                )
-        for j in range(PACK):
-            for g in range(PASSES):
-                for t in range(TIMES):
-                    x_t = banks.tile([P, BANK], BF16, name="bank")
-                    for k in range(PACK):
+                x_by_n = stage.tile([P, PACK * CHANNELS], BF16, name="x_by_n", align_bytes=64)
+                for u in range(2):
+                    x_t = banks.tile([P, BANK], F32, name="bank")
+                    for jn in range(PACK):
+                        first = (g * PACK + jn) * P
                         nc.tensor.transpose(
-                            x_t[:, k * P : (k + 1) * P],
-                            x_by_time[:, j, k, t, g * P : (g + 1) * P],
-                            ident_bf[:],
+                            x_t[:, jn * P : (jn + 1) * P], x_words[:, t, first : first + P, u], ident[:]
                         )
-                    nc.scalar.copy(out=x_by_n[g, t][:, j, :], in_=x_t[:])
-        for g in range(PASSES):
-            for t in range(TIMES):
+                    nc.scalar.copy(
+                        out=x_by_n[:, u * 2 * BANK : (u + 1) * 2 * BANK].rearrange(
+                            "p (e m jn) -> p e m jn", e=2, jn=PACK
+                        ),
+                        in_=x_t[:].bitcast(BF16).rearrange("p (jn m e) -> p e m jn", jn=PACK, e=2),
+                    )
                 nc.vector.quantize_mx(
-                    out=xn_words[:, t, g, :].bitcast(FP8X4),
-                    scales=xn_plane[:, t, g, :],
-                    in_=x_by_n[g, t][:].rearrange("p j c -> p (j c)"),
+                    out=xn_words[:, t, g, :].bitcast(FP8X4), scales=xn_plane[:, t, g, :], in_=x_by_n[:]
                 )
+
+        xc_words = keep.tile([P, TIMES, NODES], U32, align_bytes=64)
+        xc_plane = keep.tile([P, TIMES, NODES], U8, align_bytes=64)
+        for t in range(TIMES):
+            nc.vector.quantize_mx(
+                out=xc_words[:, t, :].bitcast(FP8X4),
+                scales=xc_plane[:, t, :],
+                in_=x_by_c[:, t, :, :].rearrange("p n j -> p (n j)"),
+            )
 
         deg = keep.tile([P, CHUNKS], F32)
         nc.vector.tensor_reduce(out=deg[:], in_=deg_parts[:], axis=AXIS.X, op=ALU.add)
@@ -202,19 +185,16 @@ def tile_dynamicgraphspatialconv_pa_kernel(
                 nc.tensor.transpose(r_row[:, i * P : (i + 1) * P], r_rep[:, h * (BANK // P) + i, :], ident[:])
             r_rows.append(r_row)
 
-        def scale_rows(h):
-            cols = slice(h * BANK, (h + 1) * BANK)
-            for r in range(CHUNKS):
-                if r % 3 == 0:
-                    nc.scalar.activation(
-                        out=a2[:, r, cols], in_=a2[:, r, cols], func=ACT.Copy,
-                        scale=neg_r_col[:, r : r + 1],
-                    )
-                else:
-                    nc.vector.tensor_scalar(
-                        out=a2[:, r, cols], in0=a2[:, r, cols], scalar1=neg_r_col[:, r : r + 1],
-                        scalar2=None, op0=ALU.mult,
-                    )
+        for r in range(CHUNKS):
+            if r % 3 == 0:
+                nc.scalar.activation(
+                    out=a2[:, r, :], in_=a2[:, r, :], func=ACT.Copy, scale=neg_r_col[:, r : r + 1]
+                )
+            else:
+                nc.vector.tensor_scalar(
+                    out=a2[:, r, :], in0=a2[:, r, :], scalar1=neg_r_col[:, r : r + 1], scalar2=None,
+                    op0=ALU.mult,
+                )
 
         s_words = keep.tile([P, CHUNKS, PASSES * P], U32, align_bytes=64)
         s_plane = keep.tile([P, CHUNKS, PASSES * P], U8, align_bytes=64)
@@ -226,7 +206,7 @@ def tile_dynamicgraphspatialconv_pa_kernel(
             row = r_rows[v // (BANK // P)][:, (v % (BANK // P)) * P : (v % (BANK // P) + 1) * P]
             nc.vector.tensor_tensor(
                 out=s_by_n[:],
-                in0=a2[:, :, cols].rearrange("p (jn g) q -> p g q jn", g=PASSES),
+                in0=a2[:, :, cols].rearrange("p (g jn) q -> p g q jn", g=PASSES),
                 in1=row.unsqueeze(1).unsqueeze(3).to_broadcast([P, PASSES, P, PACK]),
                 op=ALU.mult,
             )
@@ -255,7 +235,10 @@ def tile_dynamicgraphspatialconv_pa_kernel(
                         )
                 dst = tx_by_c[:, t, :].rearrange("p (q j) -> p q j", j=PACK)
                 src = tx[:].rearrange("p (j q) -> p q j", j=PACK)
-                nc.scalar.copy(out=dst, in_=src)
+                if t == TIMES - 1:
+                    nc.vector.tensor_copy(out=dst, in_=src)
+                else:
+                    nc.scalar.copy(out=dst, in_=src)
             for t in range(TIMES):
                 nc.vector.quantize_mx(
                     out=tx_words[:, t, :].bitcast(FP8X4), scales=tx_plane[:, t, :], in_=tx_by_c[:, t, :]
@@ -291,10 +274,6 @@ def tile_dynamicgraphspatialconv_pa_kernel(
             )
 
         for v in range(CHUNKS):
-            if v % (BANK // P) == 0:
-                scale_rows(v // (BANK // P))
-            if v % 2 == 0:
-                group_channels(v // 2)
             graph_columns(v)
             node_matmul(v)
             if v > 0:

@@ -23,6 +23,7 @@ BANK = 512
 HALVES = NODES // BANK
 PIECES = 4
 PIECE_NODES = NODES // PIECES
+AHEAD = 2
 
 FLOPS = 2 * TIMES * NODES * (NODES * CHANNELS + 2 * CHANNELS * OUTS)
 
@@ -33,12 +34,13 @@ def tile_dynamicgraphspatialconv_pa_kernel(
     nc = tc.nc
     with (
         tc.tile_pool(name="keep", bufs=1) as keep,
-        tc.tile_pool(name="adj_in", bufs=4) as adj_in,
+        tc.tile_pool(name="adj_in", bufs=CHUNKS) as adj_in,
         tc.tile_pool(name="x_in", bufs=PIECES) as x_in,
         tc.tile_pool(name="stage", bufs=3) as stage,
         tc.psum_pool(name="banks", bufs=4) as banks,
         tc.psum_pool(name="row_banks", bufs=1) as row_banks,
         tc.psum_pool(name="out_banks", bufs=2) as out_banks,
+        tc.manual_schedule(),
     ):
         ident = keep.tile([P, P], F32)
         make_identity(nc, ident[:])
@@ -68,6 +70,24 @@ def tile_dynamicgraphspatialconv_pa_kernel(
             nc.sync.dma_start(out=x_sb[:], in_=x_rows[:, :, i * width : (i + 1) * width])
             x_tiles.append(x_sb)
 
+        for r in range(CHUNKS // 2):
+            load_adj(r)
+        load_x(0)
+        for r in range(CHUNKS // 2, CHUNKS):
+            load_adj(r)
+        for i in range(1, PIECES):
+            load_x(i)
+        for words, plane, words_in, scales_in in weights:
+            nc.sync.dma_start(
+                out=words[:].bitcast(I32),
+                in_=words_in[0].rearrange("p n t -> p (n t)").bitcast(I32),
+            )
+            for q in range(4):
+                nc.sync.dma_start(
+                    out=plane[32 * q : 32 * q + 4, :].bitcast(I32),
+                    in_=scales_in[0, 4 * q : 4 * q + 4, :].bitcast(I32),
+                )
+
         sig = keep.tile([P, CHUNKS, NODES], F32)
 
         def sigmoid_chunk(r):
@@ -85,37 +105,29 @@ def tile_dynamicgraphspatialconv_pa_kernel(
 
         x_by_c = keep.tile([P, TIMES, NODES, PACK], BF16, align_bytes=64)
 
-        def group_channels(i):
+        def group_channels(i, t):
             nodes = slice(i * PIECE_NODES, (i + 1) * PIECE_NODES)
             src = x_tiles[i][:].rearrange("p j (n t) -> p t n j", t=TIMES)
-            nc.vector.tensor_copy(out=x_by_c[:, 0, nodes, :], in_=src[:, 0])
-            for t in range(1, TIMES):
+            if t == 0:
+                nc.scalar.copy(out=x_by_c[:, t, nodes, :], in_=src[:, t])
+            else:
                 nc.gpsimd.tensor_scalar(
                     out=x_by_c[:, t, nodes, :], in0=src[:, t], scalar1=1.0, scalar2=0.0,
                     op0=ALU.mult, op1=ALU.add,
                 )
 
-        for r in range(CHUNKS):
-            load_adj(r)
-            if r % 2 == 1:
-                load_x(r // 2)
-        for words, plane, words_in, scales_in in weights:
-            nc.sync.dma_start(
-                out=words[:].bitcast(I32),
-                in_=words_in[0].rearrange("p n t -> p (n t)").bitcast(I32),
-            )
-            for q in range(4):
-                nc.sync.dma_start(
-                    out=plane[32 * q : 32 * q + 4, :].bitcast(I32),
-                    in_=scales_in[0, 4 * q : 4 * q + 4, :].bitcast(I32),
-                )
-
-        for r in range(CHUNKS):
+        for r in range(CHUNKS // 2):
             sigmoid_chunk(r)
-            if r % 2 == 1:
-                group_channels(r // 2)
+        group_channels(0, 1)
+        group_channels(0, 2)
+        for r in range(CHUNKS // 2, CHUNKS):
+            sigmoid_chunk(r)
         warm = keep.tile([P, 1], F32)
         nc.scalar.activation(out=warm[:], in_=sig[:, CHUNKS - 1, 0:1], func=ACT.Sqrt)
+        group_channels(0, 0)
+        for i in range(1, PIECES):
+            for t in range(TIMES):
+                group_channels(i, t)
 
         a2 = keep.tile([P, CHUNKS, NODES], F32)
         deg_parts = keep.tile([P, CHUNKS, HALVES], F32)
@@ -134,73 +146,85 @@ def tile_dynamicgraphspatialconv_pa_kernel(
                     op0=ALU.mult, op1=ALU.add, accum_out=deg_parts[:, r, h : h + 1],
                 )
 
-        x_words = x_by_c[:].bitcast(F32)
-        xn_words = keep.tile([P, TIMES, PASSES, CHANNELS], U32, align_bytes=64)
-        xn_plane = keep.tile([P, TIMES, PASSES, CHANNELS], U8, align_bytes=64)
-        for g in range(PASSES):
-            for t in range(TIMES):
-                x_by_n = stage.tile([P, PACK * CHANNELS], BF16, name="x_by_n", align_bytes=64)
-                for u in range(2):
-                    x_t = banks.tile([P, BANK], F32, name="bank")
-                    for jn in range(PACK):
-                        first = (g * PACK + jn) * P
-                        nc.tensor.transpose(
-                            x_t[:, jn * P : (jn + 1) * P], x_words[:, t, first : first + P, u], ident[:]
-                        )
-                    nc.scalar.copy(
-                        out=x_by_n[:, u * 2 * BANK : (u + 1) * 2 * BANK].rearrange(
-                            "p (e m jn) -> p e m jn", e=2, jn=PACK
-                        ),
-                        in_=x_t[:].bitcast(BF16).rearrange("p (jn m e) -> p e m jn", jn=PACK, e=2),
-                    )
-                nc.vector.quantize_mx(
-                    out=xn_words[:, t, g, :].bitcast(FP8X4), scales=xn_plane[:, t, g, :], in_=x_by_n[:]
-                )
-
-        xc_words = keep.tile([P, TIMES, NODES], U32, align_bytes=64)
-        xc_plane = keep.tile([P, TIMES, NODES], U8, align_bytes=64)
-        for t in range(TIMES):
-            nc.vector.quantize_mx(
-                out=xc_words[:, t, :].bitcast(FP8X4),
-                scales=xc_plane[:, t, :],
-                in_=x_by_c[:, t, :, :].rearrange("p n j -> p (n j)"),
-            )
-
         deg = keep.tile([P, CHUNKS], F32)
         nc.vector.tensor_reduce(out=deg[:], in_=deg_parts[:], axis=AXIS.X, op=ALU.add)
         root = keep.tile([P, CHUNKS], F32)
         nc.scalar.activation(out=root[:], in_=deg[:], func=ACT.Sqrt)
         r_col = keep.tile([P, CHUNKS], F32)
         nc.vector.reciprocal(out=r_col[:], in_=root[:])
-        neg_r_col = keep.tile([P, CHUNKS], F32)
-        nc.vector.tensor_scalar(
-            out=neg_r_col[:], in0=r_col[:], scalar1=-1.0, scalar2=None, op0=ALU.mult
-        )
         r_rep = keep.tile([P, CHUNKS, P], F32)
-        nc.vector.tensor_copy(out=r_rep[:], in_=r_col[:].unsqueeze(2).to_broadcast([P, CHUNKS, P]))
-        r_rows = []
-        for h in range(HALVES):
-            r_row = row_banks.tile([P, BANK], F32, name="r_row%d" % h)
-            for i in range(BANK // P):
-                nc.tensor.transpose(r_row[:, i * P : (i + 1) * P], r_rep[:, h * (BANK // P) + i, :], ident[:])
-            r_rows.append(r_row)
+        nc.vector.tensor_scalar(
+            out=r_rep[:], in0=r_col[:].unsqueeze(2).to_broadcast([P, CHUNKS, P]), scalar1=-1.0,
+            scalar2=None, op0=ALU.mult,
+        )
 
-        for r in range(CHUNKS):
-            if r % 3 == 0:
-                nc.scalar.activation(
-                    out=a2[:, r, :], in_=a2[:, r, :], func=ACT.Copy, scale=neg_r_col[:, r : r + 1]
+        def scale_rows_first_half():
+            for r in range(CHUNKS):
+                if r % 3 == 0:
+                    nc.scalar.activation(
+                        out=a2[:, r, :BANK], in_=a2[:, r, :BANK], func=ACT.Copy,
+                        scale=r_col[:, r : r + 1],
+                    )
+                else:
+                    nc.vector.tensor_scalar(
+                        out=a2[:, r, :BANK], in0=a2[:, r, :BANK], scalar1=r_col[:, r : r + 1],
+                        scalar2=None, op0=ALU.mult,
+                    )
+
+        def scale_rows_second_half():
+            for r in range(CHUNKS):
+                nc.gpsimd.tensor_scalar(
+                    out=a2[:, r, BANK:], in0=a2[:, r, BANK:], scalar1=r_col[:, r : r + 1],
+                    scalar2=0.0, op0=ALU.mult, op1=ALU.add,
                 )
-            else:
-                nc.vector.tensor_scalar(
-                    out=a2[:, r, :], in0=a2[:, r, :], scalar1=neg_r_col[:, r : r + 1], scalar2=None,
-                    op0=ALU.mult,
+
+        x_words = x_by_c[:].bitcast(F32)
+        xn_words = keep.tile([P, TIMES, PASSES, CHANNELS], U32, align_bytes=64)
+        xn_plane = keep.tile([P, TIMES, PASSES, CHANNELS], U8, align_bytes=64)
+
+        def nodes_to_partitions(g, t):
+            x_by_n = stage.tile([P, PACK * CHANNELS], BF16, name="x_by_n", align_bytes=64)
+            for u in range(2):
+                x_t = banks.tile([P, BANK], F32, name="bank")
+                for jn in range(PACK):
+                    first = (g * PACK + jn) * P
+                    nc.tensor.transpose(
+                        x_t[:, jn * P : (jn + 1) * P], x_words[:, t, first : first + P, u], ident[:]
+                    )
+                dst = x_by_n[:, u * 2 * BANK : (u + 1) * 2 * BANK].rearrange(
+                    "p (e m jn) -> p e m jn", e=2, jn=PACK
+                )
+                src = x_t[:].bitcast(BF16).rearrange("p (jn m e) -> p e m jn", jn=PACK, e=2)
+                if g == 1 and u == 1:
+                    nc.vector.tensor_copy(out=dst, in_=src)
+                else:
+                    nc.scalar.copy(out=dst, in_=src)
+            return x_by_n
+
+        def quantise_nodes(g, t, x_by_n):
+            nc.vector.quantize_mx(
+                out=xn_words[:, t, g, :].bitcast(FP8X4), scales=xn_plane[:, t, g, :], in_=x_by_n[:]
+            )
+
+        xc_words = keep.tile([P, TIMES, NODES], U32, align_bytes=64)
+        xc_plane = keep.tile([P, TIMES, NODES], U8, align_bytes=64)
+
+        def quantise_channels(h):
+            nodes = slice(h * BANK, (h + 1) * BANK)
+            for t in range(TIMES):
+                nc.vector.quantize_mx(
+                    out=xc_words[:, t, nodes].bitcast(FP8X4),
+                    scales=xc_plane[:, t, nodes],
+                    in_=x_by_c[:, t, nodes, :].rearrange("p n j -> p (n j)"),
                 )
 
         s_words = keep.tile([P, CHUNKS, PASSES * P], U32, align_bytes=64)
         s_plane = keep.tile([P, CHUNKS, PASSES * P], U8, align_bytes=64)
+        r_rows = []
+        s_tiles = {}
         tx_tiles = {}
 
-        def graph_columns(v):
+        def scale_columns(v):
             cols = slice(v * P, (v + 1) * P)
             s_by_n = stage.tile([P, PASSES, P, PACK], BF16, name="s_by_n", align_bytes=64)
             row = r_rows[v // (BANK // P)][:, (v % (BANK // P)) * P : (v % (BANK // P) + 1) * P]
@@ -210,16 +234,17 @@ def tile_dynamicgraphspatialconv_pa_kernel(
                 in1=row.unsqueeze(1).unsqueeze(3).to_broadcast([P, PASSES, P, PACK]),
                 op=ALU.mult,
             )
+            s_tiles[v] = s_by_n
+
+        def quantise_columns(v):
             nc.vector.quantize_mx(
                 out=s_words[:, v, :].bitcast(FP8X4),
                 scales=s_plane[:, v, :],
-                in_=s_by_n[:].rearrange("p g q jn -> p (g q jn)"),
+                in_=s_tiles[v][:].rearrange("p g q jn -> p (g q jn)"),
             )
 
         def node_matmul(v):
             tx_by_c = stage.tile([P, TIMES, P * PACK], BF16, name="tx_by_c", align_bytes=64)
-            tx_words = stage.tile([P, TIMES, P], U32, name="tx_words", align_bytes=64)
-            tx_plane = stage.tile([P, TIMES, P], U8, name="tx_plane", align_bytes=64)
             for t in range(TIMES):
                 tx = banks.tile([P, BANK], F32, name="bank")
                 for j in range(PACK):
@@ -233,12 +258,16 @@ def tile_dynamicgraphspatialconv_pa_kernel(
                             start=(g == 0),
                             stop=(g == PASSES - 1),
                         )
-                dst = tx_by_c[:, t, :].rearrange("p (q j) -> p q j", j=PACK)
-                src = tx[:].rearrange("p (j q) -> p q j", j=PACK)
-                if t == TIMES - 1:
-                    nc.vector.tensor_copy(out=dst, in_=src)
-                else:
-                    nc.scalar.copy(out=dst, in_=src)
+                nc.scalar.copy(
+                    out=tx_by_c[:, t, :].rearrange("p (q j) -> p q j", j=PACK),
+                    in_=tx[:].rearrange("p (j q) -> p q j", j=PACK),
+                )
+            tx_tiles[v] = tx_by_c
+
+        def quantise_tx(v):
+            tx_by_c = tx_tiles[v]
+            tx_words = stage.tile([P, TIMES, P], U32, name="tx_words", align_bytes=64)
+            tx_plane = stage.tile([P, TIMES, P], U8, name="tx_plane", align_bytes=64)
             for t in range(TIMES):
                 nc.vector.quantize_mx(
                     out=tx_words[:, t, :].bitcast(FP8X4), scales=tx_plane[:, t, :], in_=tx_by_c[:, t, :]
@@ -273,9 +302,33 @@ def tile_dynamicgraphspatialconv_pa_kernel(
                 out=out[0, :, v * P : (v + 1) * P, :].rearrange("t q o -> q t o"), in_=result[:]
             )
 
+        scale_rows_first_half()
+        first_x = nodes_to_partitions(0, 0)
+        for h in range(HALVES):
+            r_row = row_banks.tile([P, BANK], F32, name="r_row%d" % h)
+            for i in range(BANK // P):
+                nc.tensor.transpose(r_row[:, i * P : (i + 1) * P], r_rep[:, h * (BANK // P) + i, :], ident[:])
+            r_rows.append(r_row)
+        scale_columns(0)
+        scale_columns(1)
+        quantise_columns(0)
+        quantise_columns(1)
+        quantise_nodes(0, 0, first_x)
+        for g in range(PASSES):
+            for t in range(TIMES):
+                if (g, t) != (0, 0):
+                    quantise_nodes(g, t, nodes_to_partitions(g, t))
+        scale_rows_second_half()
+
         for v in range(CHUNKS):
-            graph_columns(v)
             node_matmul(v)
+            if v + AHEAD < CHUNKS:
+                scale_columns(v + AHEAD)
+            if v < HALVES:
+                quantise_channels(v)
+            quantise_tx(v)
+            if v + AHEAD < CHUNKS:
+                quantise_columns(v + AHEAD)
             if v > 0:
                 channel_matmuls(v - 1)
         channel_matmuls(CHUNKS - 1)

@@ -105,29 +105,21 @@ def tile_dynamicgraphspatialconv_pa_kernel(
 
         x_by_c = keep.tile([P, TIMES, NODES, PACK], BF16, align_bytes=64)
 
-        def group_channels(i, t):
+        def group_channels(engine_copy, i, t):
             nodes = slice(i * PIECE_NODES, (i + 1) * PIECE_NODES)
             src = x_tiles[i][:].rearrange("p j (n t) -> p t n j", t=TIMES)
-            if t == 0:
-                nc.scalar.copy(out=x_by_c[:, t, nodes, :], in_=src[:, t])
-            else:
-                nc.gpsimd.tensor_scalar(
-                    out=x_by_c[:, t, nodes, :], in0=src[:, t], scalar1=1.0, scalar2=0.0,
-                    op0=ALU.mult, op1=ALU.add,
-                )
+            engine_copy(out=x_by_c[:, t, nodes, :], in_=src[:, t])
 
         for r in range(CHUNKS // 2):
             sigmoid_chunk(r)
-        group_channels(0, 1)
-        group_channels(0, 2)
+        for t in range(TIMES):
+            group_channels(nc.vector.tensor_copy, 0, t)
         for r in range(CHUNKS // 2, CHUNKS):
             sigmoid_chunk(r)
         warm = keep.tile([P, 1], F32)
         nc.scalar.activation(out=warm[:], in_=sig[:, CHUNKS - 1, 0:1], func=ACT.Sqrt)
-        group_channels(0, 0)
         for i in range(1, PIECES):
-            for t in range(TIMES):
-                group_channels(i, t)
+            group_channels(nc.scalar.copy, i, 0)
 
         a2 = keep.tile([P, CHUNKS, NODES], F32)
         deg_parts = keep.tile([P, CHUNKS, HALVES], F32)
@@ -157,26 +149,23 @@ def tile_dynamicgraphspatialconv_pa_kernel(
             out=r_rep[:], in0=r_col[:].unsqueeze(2).to_broadcast([P, CHUNKS, P]), scalar1=-1.0,
             scalar2=None, op0=ALU.mult,
         )
+        for i in range(1, PIECES):
+            for t in range(1, TIMES):
+                group_channels(nc.vector.tensor_copy, i, t)
 
-        def scale_rows_first_half():
+        def scale_rows(h):
+            cols = slice(h * BANK, (h + 1) * BANK)
             for r in range(CHUNKS):
                 if r % 3 == 0:
                     nc.scalar.activation(
-                        out=a2[:, r, :BANK], in_=a2[:, r, :BANK], func=ACT.Copy,
+                        out=a2[:, r, cols], in_=a2[:, r, cols], func=ACT.Copy,
                         scale=r_col[:, r : r + 1],
                     )
                 else:
                     nc.vector.tensor_scalar(
-                        out=a2[:, r, :BANK], in0=a2[:, r, :BANK], scalar1=r_col[:, r : r + 1],
+                        out=a2[:, r, cols], in0=a2[:, r, cols], scalar1=r_col[:, r : r + 1],
                         scalar2=None, op0=ALU.mult,
                     )
-
-        def scale_rows_second_half():
-            for r in range(CHUNKS):
-                nc.gpsimd.tensor_scalar(
-                    out=a2[:, r, BANK:], in0=a2[:, r, BANK:], scalar1=r_col[:, r : r + 1],
-                    scalar2=0.0, op0=ALU.mult, op1=ALU.add,
-                )
 
         x_words = x_by_c[:].bitcast(F32)
         xn_words = keep.tile([P, TIMES, PASSES, CHANNELS], U32, align_bytes=64)
@@ -302,7 +291,7 @@ def tile_dynamicgraphspatialconv_pa_kernel(
                 out=out[0, :, v * P : (v + 1) * P, :].rearrange("t q o -> q t o"), in_=result[:]
             )
 
-        scale_rows_first_half()
+        scale_rows(0)
         first_x = nodes_to_partitions(0, 0)
         for h in range(HALVES):
             r_row = row_banks.tile([P, BANK], F32, name="r_row%d" % h)
@@ -318,10 +307,11 @@ def tile_dynamicgraphspatialconv_pa_kernel(
             for t in range(TIMES):
                 if (g, t) != (0, 0):
                     quantise_nodes(g, t, nodes_to_partitions(g, t))
-        scale_rows_second_half()
 
         for v in range(CHUNKS):
             node_matmul(v)
+            if v == 0:
+                scale_rows(1)
             if v + AHEAD < CHUNKS:
                 scale_columns(v + AHEAD)
             if v < HALVES:

@@ -23,7 +23,8 @@ BANK = 512
 HALVES = NODES // BANK
 PIECES = 4
 PIECE_NODES = NODES // PIECES
-AHEAD = 2
+AHEAD = 3
+LAG = 2
 
 FLOPS = 2 * TIMES * NODES * (NODES * CHANNELS + 2 * CHANNELS * OUTS)
 
@@ -105,21 +106,29 @@ def tile_dynamicgraphspatialconv_pa_kernel(
 
         x_by_c = keep.tile([P, TIMES, NODES, PACK], BF16, align_bytes=64)
 
-        def group_channels(engine_copy, i, t):
+        def group_channels(i):
             nodes = slice(i * PIECE_NODES, (i + 1) * PIECE_NODES)
             src = x_tiles[i][:].rearrange("p j (n t) -> p t n j", t=TIMES)
-            engine_copy(out=x_by_c[:, t, nodes, :], in_=src[:, t])
+            for t in range(TIMES):
+                if i == 0:
+                    nc.vector.tensor_copy(out=x_by_c[:, t, nodes, :], in_=src[:, t])
+                elif i == PIECES - 1:
+                    nc.scalar.copy(out=x_by_c[:, t, nodes, :], in_=src[:, t])
+                else:
+                    nc.gpsimd.tensor_scalar(
+                        out=x_by_c[:, t, nodes, :], in0=src[:, t], scalar1=1.0, scalar2=0.0,
+                        op0=ALU.mult, op1=ALU.add,
+                    )
 
         for r in range(CHUNKS // 2):
             sigmoid_chunk(r)
-        for t in range(TIMES):
-            group_channels(nc.vector.tensor_copy, 0, t)
+        group_channels(0)
         for r in range(CHUNKS // 2, CHUNKS):
             sigmoid_chunk(r)
         warm = keep.tile([P, 1], F32)
         nc.scalar.activation(out=warm[:], in_=sig[:, CHUNKS - 1, 0:1], func=ACT.Sqrt)
         for i in range(1, PIECES):
-            group_channels(nc.scalar.copy, i, 0)
+            group_channels(i)
 
         a2 = keep.tile([P, CHUNKS, NODES], F32)
         deg_parts = keep.tile([P, CHUNKS, HALVES], F32)
@@ -149,23 +158,14 @@ def tile_dynamicgraphspatialconv_pa_kernel(
             out=r_rep[:], in0=r_col[:].unsqueeze(2).to_broadcast([P, CHUNKS, P]), scalar1=-1.0,
             scalar2=None, op0=ALU.mult,
         )
-        for i in range(1, PIECES):
-            for t in range(1, TIMES):
-                group_channels(nc.vector.tensor_copy, i, t)
 
         def scale_rows(h):
             cols = slice(h * BANK, (h + 1) * BANK)
             for r in range(CHUNKS):
-                if r % 3 == 0:
-                    nc.scalar.activation(
-                        out=a2[:, r, cols], in_=a2[:, r, cols], func=ACT.Copy,
-                        scale=r_col[:, r : r + 1],
-                    )
-                else:
-                    nc.vector.tensor_scalar(
-                        out=a2[:, r, cols], in0=a2[:, r, cols], scalar1=r_col[:, r : r + 1],
-                        scalar2=None, op0=ALU.mult,
-                    )
+                nc.vector.tensor_scalar(
+                    out=a2[:, r, cols], in0=a2[:, r, cols], scalar1=r_col[:, r : r + 1],
+                    scalar2=None, op0=ALU.mult,
+                )
 
         x_words = x_by_c[:].bitcast(F32)
         xn_words = keep.tile([P, TIMES, PASSES, CHANNELS], U32, align_bytes=64)
@@ -298,10 +298,10 @@ def tile_dynamicgraphspatialconv_pa_kernel(
             for i in range(BANK // P):
                 nc.tensor.transpose(r_row[:, i * P : (i + 1) * P], r_rep[:, h * (BANK // P) + i, :], ident[:])
             r_rows.append(r_row)
-        scale_columns(0)
-        scale_columns(1)
-        quantise_columns(0)
-        quantise_columns(1)
+        for v in range(AHEAD):
+            scale_columns(v)
+        for v in range(AHEAD):
+            quantise_columns(v)
         quantise_nodes(0, 0, first_x)
         for g in range(PASSES):
             for t in range(TIMES):
@@ -314,11 +314,12 @@ def tile_dynamicgraphspatialconv_pa_kernel(
                 scale_rows(1)
             if v + AHEAD < CHUNKS:
                 scale_columns(v + AHEAD)
-            if v < HALVES:
-                quantise_channels(v)
             quantise_tx(v)
             if v + AHEAD < CHUNKS:
                 quantise_columns(v + AHEAD)
-            if v > 0:
-                channel_matmuls(v - 1)
-        channel_matmuls(CHUNKS - 1)
+            if v % LAG == 0 and v // LAG < HALVES:
+                quantise_channels(v // LAG)
+            if v >= LAG:
+                channel_matmuls(v - LAG)
+        for v in range(CHUNKS - LAG, CHUNKS):
+            channel_matmuls(v)

@@ -37,7 +37,9 @@ def tile_dynamicgraphspatialconv_pa_kernel(
         tc.tile_pool(name="keep", bufs=1) as keep,
         tc.tile_pool(name="adj_in", bufs=CHUNKS) as adj_in,
         tc.tile_pool(name="x_in", bufs=PIECES) as x_in,
-        tc.tile_pool(name="stage", bufs=3) as stage,
+        tc.tile_pool(name="stage", bufs=4) as stage,
+        tc.tile_pool(name="x_stage", bufs=4) as x_stage,
+        tc.tile_pool(name="s_stage", bufs=CHUNKS) as s_stage,
         tc.psum_pool(name="banks", bufs=4) as banks,
         tc.psum_pool(name="row_banks", bufs=1) as row_banks,
         tc.psum_pool(name="out_banks", bufs=2) as out_banks,
@@ -45,6 +47,8 @@ def tile_dynamicgraphspatialconv_pa_kernel(
     ):
         ident = keep.tile([P, P], F32)
         make_identity(nc, ident[:])
+        ident_bf = keep.tile([P, P], BF16)
+        make_identity(nc, ident_bf[:])
 
         weights = []
         for name, words_in, scales_in in (
@@ -71,12 +75,15 @@ def tile_dynamicgraphspatialconv_pa_kernel(
             nc.sync.dma_start(out=x_sb[:], in_=x_rows[:, :, i * width : (i + 1) * width])
             x_tiles.append(x_sb)
 
-        for r in range(CHUNKS // 2):
+        for r in range(2):
             load_adj(r)
         load_x(0)
-        for r in range(CHUNKS // 2, CHUNKS):
+        for r in range(2, 5):
             load_adj(r)
-        for i in range(1, PIECES):
+        load_x(1)
+        for r in range(5, CHUNKS):
+            load_adj(r)
+        for i in range(2, PIECES):
             load_x(i)
         for words, plane, words_in, scales_in in weights:
             nc.sync.dma_start(
@@ -91,90 +98,82 @@ def tile_dynamicgraphspatialconv_pa_kernel(
 
         sig = keep.tile([P, CHUNKS, NODES], F32)
 
-        def sigmoid_chunk(r):
-            nc.scalar.activation(out=sig[:, r, :], in_=adj_tiles[r][:], func=ACT.Sigmoid)
-            diag = sig[:, r, r * P : (r + 1) * P]
+        def mask_diagonal(r):
+            diag = adj_tiles[r][:, r * P : (r + 1) * P]
             nc.gpsimd.affine_select(
                 out=diag,
                 in_=diag,
                 pattern=[[-1, P]],
                 compare_op=ALU.not_equal,
-                fill=0.0,
+                fill=-512.0,
                 base=0,
                 channel_multiplier=1,
             )
 
+        def sigmoid_chunk(r):
+            nc.scalar.activation(out=sig[:, r, :], in_=adj_tiles[r][:], func=ACT.Sigmoid)
+
         x_by_c = keep.tile([P, TIMES, NODES, PACK], BF16, align_bytes=64)
 
-        def group_channels(i):
+        def group_channels(i, t):
             nodes = slice(i * PIECE_NODES, (i + 1) * PIECE_NODES)
             src = x_tiles[i][:].rearrange("p j (n t) -> p t n j", t=TIMES)
-            for t in range(TIMES):
-                if i == 0:
-                    nc.vector.tensor_copy(out=x_by_c[:, t, nodes, :], in_=src[:, t])
-                elif i == PIECES - 1:
-                    nc.scalar.copy(out=x_by_c[:, t, nodes, :], in_=src[:, t])
-                else:
-                    nc.gpsimd.tensor_scalar(
-                        out=x_by_c[:, t, nodes, :], in0=src[:, t], scalar1=1.0, scalar2=0.0,
-                        op0=ALU.mult, op1=ALU.add,
-                    )
+            if i == 0:
+                nc.vector.tensor_copy(out=x_by_c[:, t, nodes, :], in_=src[:, t])
+            else:
+                nc.gpsimd.tensor_scalar(
+                    out=x_by_c[:, t, nodes, :], in0=src[:, t], scalar1=1.0, scalar2=0.0,
+                    op0=ALU.mult, op1=ALU.add,
+                )
 
-        for r in range(CHUNKS // 2):
-            sigmoid_chunk(r)
-        group_channels(0)
-        for r in range(CHUNKS // 2, CHUNKS):
-            sigmoid_chunk(r)
         warm = keep.tile([P, 1], F32)
-        nc.scalar.activation(out=warm[:], in_=sig[:, CHUNKS - 1, 0:1], func=ACT.Sqrt)
-        for i in range(1, PIECES):
-            group_channels(i)
+        nc.scalar.activation(out=warm[:], in_=ident[:, 0:1], func=ACT.Sigmoid)
+        for r in range(CHUNKS):
+            mask_diagonal(r)
+        for r in range(CHUNKS):
+            sigmoid_chunk(r)
+        nc.scalar.activation(out=warm[:], in_=ident[:, 0:1], func=ACT.Sqrt)
+        for t in range(TIMES):
+            for i in range(PIECES):
+                group_channels(i, t)
 
         a2 = keep.tile([P, CHUNKS, NODES], F32)
         deg_parts = keep.tile([P, CHUNKS, HALVES], F32)
-        for h in range(HALVES):
-            for r in range(CHUNKS):
-                sig_t = banks.tile([P, BANK], F32, name="bank")
-                for i in range(BANK // P):
-                    nc.tensor.transpose(
-                        sig_t[:, i * P : (i + 1) * P],
-                        sig[:, h * (BANK // P) + i, r * P : (r + 1) * P],
-                        ident[:],
-                    )
-                cols = slice(h * BANK, (h + 1) * BANK)
-                nc.vector.scalar_tensor_tensor(
-                    out=a2[:, r, cols], in0=sig[:, r, cols], scalar=1.0, in1=sig_t[:],
-                    op0=ALU.mult, op1=ALU.add, accum_out=deg_parts[:, r, h : h + 1],
+        ones = keep.tile([P, 1], F32)
+        nc.vector.memset(ones[:], 1.0)
+
+        def add_transposed(r, h):
+            sig_t = banks.tile([P, BANK], F32, name="bank")
+            for i in range(BANK // P):
+                nc.tensor.transpose(
+                    sig_t[:, i * P : (i + 1) * P],
+                    sig[:, h * (BANK // P) + i, r * P : (r + 1) * P],
+                    ident[:],
                 )
-
-        deg = keep.tile([P, CHUNKS], F32)
-        nc.vector.tensor_reduce(out=deg[:], in_=deg_parts[:], axis=AXIS.X, op=ALU.add)
-        root = keep.tile([P, CHUNKS], F32)
-        nc.scalar.activation(out=root[:], in_=deg[:], func=ACT.Sqrt)
-        r_col = keep.tile([P, CHUNKS], F32)
-        nc.vector.reciprocal(out=r_col[:], in_=root[:])
-        r_rep = keep.tile([P, CHUNKS, P], F32)
-        nc.vector.tensor_scalar(
-            out=r_rep[:], in0=r_col[:].unsqueeze(2).to_broadcast([P, CHUNKS, P]), scalar1=-1.0,
-            scalar2=None, op0=ALU.mult,
-        )
-
-        def scale_rows(h):
             cols = slice(h * BANK, (h + 1) * BANK)
-            for r in range(CHUNKS):
+            nc.vector.scalar_tensor_tensor(
+                out=a2[:, r, cols], in0=sig[:, r, cols], scalar=1.0, in1=sig_t[:],
+                op0=ALU.mult, op1=ALU.add, accum_out=deg_parts[:, r, h : h + 1],
+            )
+
+        def scale_rows(rows, first, width):
+            cols = slice(first, first + width)
+            for r in rows:
                 nc.vector.tensor_scalar(
                     out=a2[:, r, cols], in0=a2[:, r, cols], scalar1=r_col[:, r : r + 1],
-                    scalar2=None, op0=ALU.mult,
+                    scalar2=-1.0, op0=ALU.mult, op1=ALU.mult,
                 )
 
         x_words = x_by_c[:].bitcast(F32)
         xn_words = keep.tile([P, TIMES, PASSES, CHANNELS], U32, align_bytes=64)
         xn_plane = keep.tile([P, TIMES, PASSES, CHANNELS], U8, align_bytes=64)
 
+        x_by_n_tiles = {}
+
         def nodes_to_partitions(g, t):
-            x_by_n = stage.tile([P, PACK * CHANNELS], BF16, name="x_by_n", align_bytes=64)
+            x_by_n = x_stage.tile([P, PACK * CHANNELS], BF16, name="x_by_n", align_bytes=64)
             for u in range(2):
-                x_t = banks.tile([P, BANK], F32, name="bank")
+                x_t = out_banks.tile([P, BANK], F32, name="acc")
                 for jn in range(PACK):
                     first = (g * PACK + jn) * P
                     nc.tensor.transpose(
@@ -184,46 +183,60 @@ def tile_dynamicgraphspatialconv_pa_kernel(
                     "p (e m jn) -> p e m jn", e=2, jn=PACK
                 )
                 src = x_t[:].bitcast(BF16).rearrange("p (jn m e) -> p e m jn", jn=PACK, e=2)
-                if g == 1 and u == 1:
-                    nc.vector.tensor_copy(out=dst, in_=src)
-                else:
-                    nc.scalar.copy(out=dst, in_=src)
-            return x_by_n
+                nc.scalar.copy(out=dst, in_=src)
+            x_by_n_tiles[g, t] = x_by_n
 
-        def quantise_nodes(g, t, x_by_n):
+        def quantise_nodes(g, t):
             nc.vector.quantize_mx(
-                out=xn_words[:, t, g, :].bitcast(FP8X4), scales=xn_plane[:, t, g, :], in_=x_by_n[:]
+                out=xn_words[:, t, g, :].bitcast(FP8X4),
+                scales=xn_plane[:, t, g, :],
+                in_=x_by_n_tiles[g, t][:],
             )
 
         xc_words = keep.tile([P, TIMES, NODES], U32, align_bytes=64)
         xc_plane = keep.tile([P, TIMES, NODES], U8, align_bytes=64)
 
-        def quantise_channels(h):
+        def quantise_channels(t, h):
             nodes = slice(h * BANK, (h + 1) * BANK)
-            for t in range(TIMES):
-                nc.vector.quantize_mx(
-                    out=xc_words[:, t, nodes].bitcast(FP8X4),
-                    scales=xc_plane[:, t, nodes],
-                    in_=x_by_c[:, t, nodes, :].rearrange("p n j -> p (n j)"),
-                )
+            nc.vector.quantize_mx(
+                out=xc_words[:, t, nodes].bitcast(FP8X4),
+                scales=xc_plane[:, t, nodes],
+                in_=x_by_c[:, t, nodes, :].rearrange("p n j -> p (n j)"),
+            )
 
         s_words = keep.tile([P, CHUNKS, PASSES * P], U32, align_bytes=64)
         s_plane = keep.tile([P, CHUNKS, PASSES * P], U8, align_bytes=64)
         r_rows = []
-        s_tiles = {}
+        s_tiles = []
+        for v in range(CHUNKS):
+            s_by_n = s_stage.tile([P, PASSES, P, PACK], BF16, name="s_by_n", align_bytes=64)
+            s_tiles.append(s_by_n)
         tx_tiles = {}
 
         def scale_columns(v):
             cols = slice(v * P, (v + 1) * P)
-            s_by_n = stage.tile([P, PASSES, P, PACK], BF16, name="s_by_n", align_bytes=64)
-            row = r_rows[v // (BANK // P)][:, (v % (BANK // P)) * P : (v % (BANK // P) + 1) * P]
-            nc.vector.tensor_tensor(
-                out=s_by_n[:],
-                in0=a2[:, :, cols].rearrange("p (g jn) q -> p g q jn", g=PASSES),
-                in1=row.unsqueeze(1).unsqueeze(3).to_broadcast([P, PASSES, P, PACK]),
-                op=ALU.mult,
-            )
-            s_tiles[v] = s_by_n
+            s_by_n = s_tiles[v]
+            row = r_rows[v // PACK][:, (v % PACK) * P : (v % PACK + 1) * P]
+            if v < PACK:
+                nc.vector.tensor_tensor(
+                    out=s_by_n[:],
+                    in0=a2[:, :, cols].rearrange("p (g jn) q -> p g q jn", g=PASSES),
+                    in1=row.unsqueeze(1).unsqueeze(3).to_broadcast([P, PASSES, P, PACK]),
+                    op=ALU.mult,
+                )
+            else:
+                nc.vector.tensor_tensor(
+                    out=s_by_n[:, 1],
+                    in0=a2[:, PACK:, cols].rearrange("p jn q -> p q jn"),
+                    in1=row.unsqueeze(2).to_broadcast([P, P, PACK]),
+                    op=ALU.mult,
+                )
+
+        def mirror(v):
+            s_t = banks.tile([P, PACK, P], BF16, name="bank")
+            for jn in range(PACK):
+                nc.tensor.transpose(s_t[:, jn, :], s_tiles[jn][:, 1, :, v - PACK], ident_bf[:])
+            nc.vector.tensor_copy(out=s_tiles[v][:, 0], in_=s_t[:].rearrange("p jn q -> p q jn"))
 
         def quantise_columns(v):
             nc.vector.quantize_mx(
@@ -232,26 +245,27 @@ def tile_dynamicgraphspatialconv_pa_kernel(
                 in_=s_tiles[v][:].rearrange("p g q jn -> p (g q jn)"),
             )
 
-        def node_matmul(v):
-            tx_by_c = stage.tile([P, TIMES, P * PACK], BF16, name="tx_by_c", align_bytes=64)
-            for t in range(TIMES):
-                tx = banks.tile([P, BANK], F32, name="bank")
-                for j in range(PACK):
-                    for g in range(PASSES):
-                        nc.tensor.matmul_mx(
-                            out=tx[:, j * P : (j + 1) * P],
-                            lhsT=xn_words[:, t, g, j * P : (j + 1) * P].bitcast(FP8X4),
-                            lhsT_scale=xn_plane[:, t, g, j * P : (j + 1) * P],
-                            rhs=s_words[:, v, g * P : (g + 1) * P].bitcast(FP8X4),
-                            rhs_scale=s_plane[:, v, g * P : (g + 1) * P],
-                            start=(g == 0),
-                            stop=(g == PASSES - 1),
-                        )
-                nc.scalar.copy(
-                    out=tx_by_c[:, t, :].rearrange("p (q j) -> p q j", j=PACK),
-                    in_=tx[:].rearrange("p (j q) -> p q j", j=PACK),
-                )
-            tx_tiles[v] = tx_by_c
+        def node_matmul(v, t):
+            if t == 0:
+                tx_by_c = stage.tile([P, TIMES, P * PACK], BF16, name="tx_by_c", align_bytes=64)
+                tx_tiles[v] = tx_by_c
+            tx_by_c = tx_tiles[v]
+            tx = banks.tile([P, BANK], F32, name="bank")
+            for j in range(PACK):
+                for g in range(PASSES):
+                    nc.tensor.matmul_mx(
+                        out=tx[:, j * P : (j + 1) * P],
+                        lhsT=xn_words[:, t, g, j * P : (j + 1) * P].bitcast(FP8X4),
+                        lhsT_scale=xn_plane[:, t, g, j * P : (j + 1) * P],
+                        rhs=s_words[:, v, g * P : (g + 1) * P].bitcast(FP8X4),
+                        rhs_scale=s_plane[:, v, g * P : (g + 1) * P],
+                        start=(g == 0),
+                        stop=(g == PASSES - 1),
+                    )
+            nc.scalar.copy(
+                out=tx_by_c[:, t, :].rearrange("p (q j) -> p q j", j=PACK),
+                in_=tx[:].rearrange("p (j q) -> p q j", j=PACK),
+            )
 
         def quantise_tx(v):
             tx_by_c = tx_tiles[v]
@@ -291,35 +305,87 @@ def tile_dynamicgraphspatialconv_pa_kernel(
                 out=out[0, :, v * P : (v + 1) * P, :].rearrange("t q o -> q t o"), in_=result[:]
             )
 
-        scale_rows(0)
-        first_x = nodes_to_partitions(0, 0)
+        for r in range(CHUNKS):
+            add_transposed(r, 0)
+        for r in range(PACK, CHUNKS):
+            add_transposed(r, 1)
+        col_sums = row_banks.tile([P, PACK], F32, name="r_row1")
+        for c in range(PACK):
+            for r in range(PACK, CHUNKS):
+                nc.tensor.matmul(
+                    col_sums[:, c : c + 1], lhsT=a2[:, r, c * P : (c + 1) * P], rhs=ones[:],
+                    start=(r == PACK), stop=(r == CHUNKS - 1),
+                )
+        nodes_to_partitions(0, 0)
+
+        deg = keep.tile([P, CHUNKS], F32)
+        nc.vector.tensor_tensor(
+            out=deg[:, :PACK], in0=deg_parts[:, :PACK, 0], in1=col_sums[:], op=ALU.add
+        )
+        nc.vector.tensor_tensor(
+            out=deg[:, PACK:], in0=deg_parts[:, PACK:, 0], in1=deg_parts[:, PACK:, 1], op=ALU.add
+        )
+        root = keep.tile([P, CHUNKS], F32)
+        nc.scalar.activation(out=root[:], in_=deg[:], func=ACT.Sqrt)
+        r_col = keep.tile([P, CHUNKS], F32)
+        nc.vector.reciprocal(out=r_col[:], in_=root[:])
         for h in range(HALVES):
             r_row = row_banks.tile([P, BANK], F32, name="r_row%d" % h)
             for i in range(BANK // P):
-                nc.tensor.transpose(r_row[:, i * P : (i + 1) * P], r_rep[:, h * (BANK // P) + i, :], ident[:])
+                r = h * (BANK // P) + i
+                nc.tensor.transpose(
+                    r_row[:, i * P : (i + 1) * P], r_col[:, r : r + 1].to_broadcast([P, P]), ident[:]
+                )
             r_rows.append(r_row)
+        nodes_to_partitions(1, 0)
+        scale_rows(range(CHUNKS), 0, BANK // 2)
+        scale_columns(0)
+        quantise_nodes(0, 0)
+        quantise_columns(0)
+        quantise_nodes(1, 0)
+        node_matmul(0, 0)
+        nodes_to_partitions(0, 1)
+        scale_columns(1)
+        quantise_columns(1)
+        node_matmul(1, 0)
+        nodes_to_partitions(1, 1)
+        scale_rows(range(CHUNKS), BANK // 2, BANK // 2)
+        quantise_nodes(0, 1)
+        scale_columns(2)
+        quantise_nodes(1, 1)
+        quantise_columns(2)
+        node_matmul(0, 1)
+        nodes_to_partitions(0, 2)
+        node_matmul(1, 1)
+        node_matmul(2, 0)
+        nodes_to_partitions(1, 2)
+        node_matmul(2, 1)
+        scale_columns(3)
+        quantise_nodes(0, 2)
+        quantise_columns(3)
+        quantise_nodes(1, 2)
+        scale_rows(range(PACK, CHUNKS), BANK, BANK)
         for v in range(AHEAD):
-            scale_columns(v)
-        for v in range(AHEAD):
-            quantise_columns(v)
-        quantise_nodes(0, 0, first_x)
-        for g in range(PASSES):
-            for t in range(TIMES):
-                if (g, t) != (0, 0):
-                    quantise_nodes(g, t, nodes_to_partitions(g, t))
-
-        for v in range(CHUNKS):
-            node_matmul(v)
-            if v == 0:
-                scale_rows(1)
-            if v + AHEAD < CHUNKS:
-                scale_columns(v + AHEAD)
+            node_matmul(v, 2)
             quantise_tx(v)
-            if v + AHEAD < CHUNKS:
-                quantise_columns(v + AHEAD)
-            if v % LAG == 0 and v // LAG < HALVES:
-                quantise_channels(v // LAG)
-            if v >= LAG:
-                channel_matmuls(v - LAG)
-        for v in range(CHUNKS - LAG, CHUNKS):
+            if v == 0:
+                mirror(4)
+                mirror(5)
+            quantise_channels(v, 0)
+
+        for v in range(AHEAD, CHUNKS):
+            for t in range(TIMES):
+                node_matmul(v, t)
+            if v == AHEAD:
+                mirror(6)
+                mirror(7)
+            if v + 1 < CHUNKS:
+                scale_columns(v + 1)
+            channel_matmuls(v - AHEAD)
+            if v + 1 < CHUNKS:
+                quantise_columns(v + 1)
+            quantise_tx(v)
+            if v - AHEAD < TIMES:
+                quantise_channels(v - AHEAD, 1)
+        for v in range(CHUNKS - AHEAD, CHUNKS):
             channel_matmuls(v)

@@ -36,9 +36,8 @@ def tile_dynamicgraphspatialconv_pa_kernel(
     with (
         tc.tile_pool(name="keep", bufs=1) as keep,
         tc.tile_pool(name="adj_in", bufs=CHUNKS) as adj_in,
-        tc.tile_pool(name="x_in", bufs=PIECES) as x_in,
         tc.tile_pool(name="stage", bufs=4) as stage,
-        tc.tile_pool(name="x_stage", bufs=4) as x_stage,
+        tc.tile_pool(name="x_stage", bufs=6) as x_stage,
         tc.tile_pool(name="s_stage", bufs=CHUNKS) as s_stage,
         tc.psum_pool(name="banks", bufs=4) as banks,
         tc.psum_pool(name="row_banks", bufs=1) as row_banks,
@@ -62,29 +61,25 @@ def tile_dynamicgraphspatialconv_pa_kernel(
 
         x_rows = x[0].rearrange("(p j) n t -> p j (n t)", j=PACK)
         adj_tiles = []
-        x_tiles = []
+        x_sb = keep.tile([P, PACK, NODES * TIMES], BF16)
 
         def load_adj(r):
             adj_sb = adj_in.tile([P, NODES], BF16, name="adj_sb")
             nc.sync.dma_start(out=adj_sb[:], in_=adj_param[r * P : (r + 1) * P, :])
             adj_tiles.append(adj_sb)
 
-        def load_x(i):
-            width = PIECE_NODES * TIMES
-            x_sb = x_in.tile([P, PACK, width], BF16, name="x_sb")
-            nc.sync.dma_start(out=x_sb[:], in_=x_rows[:, :, i * width : (i + 1) * width])
-            x_tiles.append(x_sb)
+        def load_x(g, u):
+            cols = slice(g * BANK * TIMES, (g + 1) * BANK * TIMES)
+            rows = slice(2 * u, 2 * u + 2)
+            nc.sync.dma_start(out=x_sb[:, rows, cols], in_=x_rows[:, rows, cols])
 
-        for r in range(2):
+        for r in range(3):
             load_adj(r)
-        load_x(0)
-        for r in range(2, 5):
+        load_x(0, 0)
+        for r in range(3, CHUNKS):
             load_adj(r)
-        load_x(1)
-        for r in range(5, CHUNKS):
-            load_adj(r)
-        for i in range(2, PIECES):
-            load_x(i)
+        for g, u in ((0, 1), (1, 0), (1, 1)):
+            load_x(g, u)
         for words, plane, words_in, scales_in in weights:
             nc.sync.dma_start(
                 out=words[:].bitcast(I32),
@@ -99,61 +94,77 @@ def tile_dynamicgraphspatialconv_pa_kernel(
         sig = keep.tile([P, CHUNKS, NODES], F32)
 
         def mask_diagonal(r):
-            diag = adj_tiles[r][:, r * P : (r + 1) * P]
+            source, fill = (sig[:, r, :], 0.0) if r == 0 else (adj_tiles[r], -512.0)
+            diag = source[:, r * P : (r + 1) * P]
             nc.gpsimd.affine_select(
                 out=diag,
                 in_=diag,
                 pattern=[[-1, P]],
                 compare_op=ALU.not_equal,
-                fill=-512.0,
+                fill=fill,
                 base=0,
                 channel_multiplier=1,
             )
 
+        row_rest = keep.tile([P, PACK, 2], F32)
+
         def sigmoid_chunk(r):
-            nc.scalar.activation(out=sig[:, r, :], in_=adj_tiles[r][:], func=ACT.Sigmoid)
+            if r >= PACK:
+                nc.scalar.activation(out=sig[:, r, :], in_=adj_tiles[r][:], func=ACT.Sigmoid)
+                return
+            nc.scalar.activation(out=sig[:, r, :BANK], in_=adj_tiles[r][:, :BANK], func=ACT.Sigmoid)
+            nc.scalar.activation(
+                out=sig[:, r, BANK:], in_=adj_tiles[r][:, BANK:], func=ACT.Sigmoid,
+                accum_out=row_rest[:, r, 0:1],
+            )
 
         x_by_c = keep.tile([P, TIMES, NODES, PACK], BF16, align_bytes=64)
 
+        x_by_t = x_sb[:].rearrange("p j (n t) -> p t j n", t=TIMES)
+
         def group_channels(i, t):
             nodes = slice(i * PIECE_NODES, (i + 1) * PIECE_NODES)
-            src = x_tiles[i][:].rearrange("p j (n t) -> p t n j", t=TIMES)
-            if i == 0:
-                nc.vector.tensor_copy(out=x_by_c[:, t, nodes, :], in_=src[:, t])
-            else:
-                nc.gpsimd.tensor_scalar(
-                    out=x_by_c[:, t, nodes, :], in0=src[:, t], scalar1=1.0, scalar2=0.0,
-                    op0=ALU.mult, op1=ALU.add,
-                )
+            nc.gpsimd.tensor_scalar(
+                out=x_by_c[:, t, nodes, :], in0=x_by_t[:, t, :, nodes].rearrange("p j n -> p n j"),
+                scalar1=1.0, scalar2=0.0, op0=ALU.mult, op1=ALU.add,
+            )
 
         warm = keep.tile([P, 1], F32)
-        nc.scalar.activation(out=warm[:], in_=ident[:, 0:1], func=ACT.Sigmoid)
-        for r in range(CHUNKS):
+        nc.vector.memset(warm[:], 0.0)
+        nc.scalar.activation(out=warm[:], in_=warm[:], func=ACT.Sigmoid)
+        for r in range(1, CHUNKS):
             mask_diagonal(r)
-        for r in range(CHUNKS):
+            if r == 1:
+                sigmoid_chunk(0)
+            if r == 2:
+                mask_diagonal(0)
             sigmoid_chunk(r)
-        nc.scalar.activation(out=warm[:], in_=ident[:, 0:1], func=ACT.Sqrt)
-        for t in range(TIMES):
-            for i in range(PIECES):
-                group_channels(i, t)
-
         a2 = keep.tile([P, CHUNKS, NODES], F32)
         deg_parts = keep.tile([P, CHUNKS, HALVES], F32)
-        ones = keep.tile([P, 1], F32)
-        nc.vector.memset(ones[:], 1.0)
+        nc.vector.memset(deg_parts[:], 0.0)
 
-        def add_transposed(r, h):
+        def add_transposed(r, first, count, part):
             sig_t = banks.tile([P, BANK], F32, name="bank")
-            for i in range(BANK // P):
+            for i in range(count):
                 nc.tensor.transpose(
-                    sig_t[:, i * P : (i + 1) * P],
-                    sig[:, h * (BANK // P) + i, r * P : (r + 1) * P],
-                    ident[:],
+                    sig_t[:, i * P : (i + 1) * P], sig[:, first + i, r * P : (r + 1) * P], ident[:]
                 )
-            cols = slice(h * BANK, (h + 1) * BANK)
+            cols = slice(first * P, (first + count) * P)
             nc.vector.scalar_tensor_tensor(
-                out=a2[:, r, cols], in0=sig[:, r, cols], scalar=1.0, in1=sig_t[:],
-                op0=ALU.mult, op1=ALU.add, accum_out=deg_parts[:, r, h : h + 1],
+                out=a2[:, r, cols], in0=sig[:, r, cols], scalar=1.0, in1=sig_t[:, : count * P],
+                op0=ALU.mult, op1=ALU.add, accum_out=deg_parts[:, r, part : part + 1],
+            )
+
+        junk = keep.tile([P, BANK], F32)
+
+        def sum_transposed(r):
+            sig_t = row_banks.tile([P, BANK], F32, name="r_row%d" % (r % 2))
+            for i in range(PACK):
+                nc.tensor.transpose(
+                    sig_t[:, i * P : (i + 1) * P], sig[:, PACK + i, r * P : (r + 1) * P], ident[:]
+                )
+            nc.scalar.activation(
+                out=junk[:], in_=sig_t[:], func=ACT.Copy, accum_out=row_rest[:, r, 1:2]
             )
 
         def scale_rows(rows, first, width):
@@ -164,40 +175,46 @@ def tile_dynamicgraphspatialconv_pa_kernel(
                     scalar2=-1.0, op0=ALU.mult, op1=ALU.mult,
                 )
 
-        x_words = x_by_c[:].bitcast(F32)
         xn_words = keep.tile([P, TIMES, PASSES, CHANNELS], U32, align_bytes=64)
         xn_plane = keep.tile([P, TIMES, PASSES, CHANNELS], U8, align_bytes=64)
 
         x_by_n_tiles = {}
 
-        def nodes_to_partitions(g, t):
-            x_by_n = x_stage.tile([P, PACK * CHANNELS], BF16, name="x_by_n", align_bytes=64)
-            for u in range(2):
-                x_t = out_banks.tile([P, BANK], F32, name="acc")
+        x_banks = {}
+
+        def turn_x(g, t, u, pool=out_banks, tag="acc"):
+            x_t = pool.tile([P, 2, PACK, P], BF16, name=tag)
+            for jj in range(2):
                 for jn in range(PACK):
                     first = (g * PACK + jn) * P
                     nc.tensor.transpose(
-                        x_t[:, jn * P : (jn + 1) * P], x_words[:, t, first : first + P, u], ident[:]
+                        x_t[:, jj, jn, :], x_by_t[:, t, 2 * u + jj, first : first + P], ident_bf[:]
                     )
-                dst = x_by_n[:, u * 2 * BANK : (u + 1) * 2 * BANK].rearrange(
-                    "p (e m jn) -> p e m jn", e=2, jn=PACK
-                )
-                src = x_t[:].bitcast(BF16).rearrange("p (jn m e) -> p e m jn", jn=PACK, e=2)
+            x_banks[g, t, u] = x_t
+
+        def copy_x(g, t, u, engine="scalar"):
+            if (g, t) not in x_by_n_tiles:
+                x_by_n = x_stage.tile([P, PACK, P, PACK], BF16, name="x_by_n", align_bytes=64)
+                x_by_n_tiles[g, t] = x_by_n
+            dst = x_by_n_tiles[g, t][:, 2 * u : 2 * u + 2]
+            src = x_banks[g, t, u][:].rearrange("p jj jn m -> p jj m jn")
+            if engine == "scalar":
                 nc.scalar.copy(out=dst, in_=src)
-            x_by_n_tiles[g, t] = x_by_n
+            else:
+                nc.vector.tensor_copy(out=dst, in_=src)
 
         def quantise_nodes(g, t):
             nc.vector.quantize_mx(
                 out=xn_words[:, t, g, :].bitcast(FP8X4),
                 scales=xn_plane[:, t, g, :],
-                in_=x_by_n_tiles[g, t][:],
+                in_=x_by_n_tiles[g, t][:].rearrange("p j m jn -> p (j m jn)"),
             )
 
         xc_words = keep.tile([P, TIMES, NODES], U32, align_bytes=64)
         xc_plane = keep.tile([P, TIMES, NODES], U8, align_bytes=64)
 
-        def quantise_channels(t, h):
-            nodes = slice(h * BANK, (h + 1) * BANK)
+        def quantise_channels(t, i):
+            nodes = slice(i * PIECE_NODES, (i + 1) * PIECE_NODES)
             nc.vector.quantize_mx(
                 out=xc_words[:, t, nodes].bitcast(FP8X4),
                 scales=xc_plane[:, t, nodes],
@@ -232,11 +249,15 @@ def tile_dynamicgraphspatialconv_pa_kernel(
                     op=ALU.mult,
                 )
 
-        def mirror(v):
+        def mirror(v, engine="scalar"):
             s_t = banks.tile([P, PACK, P], BF16, name="bank")
             for jn in range(PACK):
                 nc.tensor.transpose(s_t[:, jn, :], s_tiles[jn][:, 1, :, v - PACK], ident_bf[:])
-            nc.vector.tensor_copy(out=s_tiles[v][:, 0], in_=s_t[:].rearrange("p jn q -> p q jn"))
+            dst, src = s_tiles[v][:, 0], s_t[:].rearrange("p jn q -> p q jn")
+            if engine == "scalar":
+                nc.scalar.copy(out=dst, in_=src)
+            else:
+                nc.vector.tensor_copy(out=dst, in_=src)
 
         def quantise_columns(v):
             nc.vector.quantize_mx(
@@ -305,28 +326,42 @@ def tile_dynamicgraphspatialconv_pa_kernel(
                 out=out[0, :, v * P : (v + 1) * P, :].rearrange("t q o -> q t o"), in_=result[:]
             )
 
-        for r in range(CHUNKS):
-            add_transposed(r, 0)
+        for t in range(TIMES):
+            turn_x(0, t, 0)
+            copy_x(0, t, 0, "vector")
+            if t < 2:
+                for r in range(2):
+                    add_transposed(r, 2 * t, 2, t)
+        for r in range(2, PACK):
+            add_transposed(r, 0, PACK, 0)
+        for t in range(TIMES):
+            group_channels(0, t)
         for r in range(PACK, CHUNKS):
-            add_transposed(r, 1)
-        col_sums = row_banks.tile([P, PACK], F32, name="r_row1")
-        for c in range(PACK):
-            for r in range(PACK, CHUNKS):
-                nc.tensor.matmul(
-                    col_sums[:, c : c + 1], lhsT=a2[:, r, c * P : (c + 1) * P], rhs=ones[:],
-                    start=(r == PACK), stop=(r == CHUNKS - 1),
-                )
-        nodes_to_partitions(0, 0)
+            if r >= 6:
+                sum_transposed(r - 6)
+            add_transposed(r, 0, PACK, 0)
+        for r in range(PACK, CHUNKS):
+            if r < 6:
+                sum_transposed(r - 2)
+            add_transposed(r, PACK, PACK, 1)
+        turn_x(0, 0, 1)
+        turn_x(1, 0, 0)
+        nc.scalar.activation(out=warm[:], in_=warm[:], func=ACT.Sqrt)
+        for i in range(1, PIECES):
+            for t in range(TIMES):
+                group_channels(i, t)
+        turn_x(1, 0, 1, banks, "bank")
+        turn_x(0, 1, 1, banks, "bank")
+        copy_x(0, 0, 1)
 
         deg = keep.tile([P, CHUNKS], F32)
-        nc.vector.tensor_tensor(
-            out=deg[:, :PACK], in0=deg_parts[:, :PACK, 0], in1=col_sums[:], op=ALU.add
-        )
-        nc.vector.tensor_tensor(
-            out=deg[:, PACK:], in0=deg_parts[:, PACK:, 0], in1=deg_parts[:, PACK:, 1], op=ALU.add
-        )
+        nc.vector.tensor_reduce(out=deg[:], in_=deg_parts[:], axis=AXIS.X, op=ALU.add)
+        rest = keep.tile([P, PACK], F32)
+        nc.vector.tensor_reduce(out=rest[:], in_=row_rest[:], axis=AXIS.X, op=ALU.add)
+        nc.vector.tensor_tensor(out=deg[:, :PACK], in0=deg[:, :PACK], in1=rest[:], op=ALU.add)
         root = keep.tile([P, CHUNKS], F32)
         nc.scalar.activation(out=root[:], in_=deg[:], func=ACT.Sqrt)
+        quantise_nodes(0, 0)
         r_col = keep.tile([P, CHUNKS], F32)
         nc.vector.reciprocal(out=r_col[:], in_=root[:])
         for h in range(HALVES):
@@ -337,55 +372,61 @@ def tile_dynamicgraphspatialconv_pa_kernel(
                     r_row[:, i * P : (i + 1) * P], r_col[:, r : r + 1].to_broadcast([P, P]), ident[:]
                 )
             r_rows.append(r_row)
-        nodes_to_partitions(1, 0)
-        scale_rows(range(CHUNKS), 0, BANK // 2)
+        copy_x(1, 0, 0)
+        copy_x(1, 0, 1)
+        copy_x(0, 1, 1)
+        turn_x(1, 1, 0)
+        turn_x(1, 1, 1)
+        copy_x(1, 1, 0)
+        copy_x(1, 1, 1)
+        scale_rows(range(CHUNKS), 0, P)
         scale_columns(0)
-        quantise_nodes(0, 0)
-        quantise_columns(0)
         quantise_nodes(1, 0)
+        quantise_columns(0)
         node_matmul(0, 0)
-        nodes_to_partitions(0, 1)
+        scale_rows(range(CHUNKS), P, BANK - P)
         scale_columns(1)
-        quantise_columns(1)
-        node_matmul(1, 0)
-        nodes_to_partitions(1, 1)
-        scale_rows(range(CHUNKS), BANK // 2, BANK // 2)
         quantise_nodes(0, 1)
-        scale_columns(2)
+        quantise_columns(1)
         quantise_nodes(1, 1)
-        quantise_columns(2)
+        turn_x(0, 2, 1)
+        turn_x(1, 2, 0)
+        copy_x(0, 2, 1)
+        node_matmul(1, 0)
+        copy_x(1, 2, 0)
         node_matmul(0, 1)
-        nodes_to_partitions(0, 2)
+        turn_x(1, 2, 1)
+        copy_x(1, 2, 1)
         node_matmul(1, 1)
-        node_matmul(2, 0)
-        nodes_to_partitions(1, 2)
-        node_matmul(2, 1)
-        scale_columns(3)
+        scale_columns(2)
         quantise_nodes(0, 2)
-        quantise_columns(3)
+        quantise_columns(2)
         quantise_nodes(1, 2)
-        scale_rows(range(PACK, CHUNKS), BANK, BANK)
-        for v in range(AHEAD):
+        scale_columns(3)
+        for v in range(2):
             node_matmul(v, 2)
-            quantise_tx(v)
-            if v == 0:
-                mirror(4)
-                mirror(5)
-            quantise_channels(v, 0)
+        quantise_channels(0, 0)
+        quantise_channels(1, 0)
+        quantise_columns(3)
+        quantise_tx(0)
+        quantise_channels(2, 0)
+        scale_rows(range(PACK, CHUNKS), BANK, BANK)
 
-        for v in range(AHEAD, CHUNKS):
+        for v in range(2, CHUNKS):
             for t in range(TIMES):
                 node_matmul(v, t)
-            if v == AHEAD:
-                mirror(6)
-                mirror(7)
-            if v + 1 < CHUNKS:
-                scale_columns(v + 1)
-            channel_matmuls(v - AHEAD)
-            if v + 1 < CHUNKS:
-                quantise_columns(v + 1)
-            quantise_tx(v)
-            if v - AHEAD < TIMES:
-                quantise_channels(v - AHEAD, 1)
-        for v in range(CHUNKS - AHEAD, CHUNKS):
-            channel_matmuls(v)
+            if v < 4:
+                mirror(2 * v)
+                mirror(2 * v + 1)
+            channel_matmuls(v - 2)
+            if v + 2 < CHUNKS:
+                scale_columns(v + 2)
+            quantise_tx(v - 1)
+            if v + 2 < CHUNKS:
+                quantise_columns(v + 2)
+            if v < 5:
+                for t in range(TIMES):
+                    quantise_channels(t, v - 1)
+        channel_matmuls(CHUNKS - 2)
+        quantise_tx(CHUNKS - 1)
+        channel_matmuls(CHUNKS - 1)

@@ -37,6 +37,7 @@ def tile_dynamicgraphspatialconv_pa_kernel(
         tc.tile_pool(name="keep", bufs=1) as keep,
         tc.tile_pool(name="adj_in", bufs=CHUNKS) as adj_in,
         tc.tile_pool(name="stage", bufs=4) as stage,
+        tc.tile_pool(name="x_in", bufs=PASSES) as x_in,
         tc.tile_pool(name="x_stage", bufs=6) as x_stage,
         tc.tile_pool(name="s_stage", bufs=CHUNKS) as s_stage,
         tc.psum_pool(name="banks", bufs=4) as banks,
@@ -61,7 +62,10 @@ def tile_dynamicgraphspatialconv_pa_kernel(
 
         x_rows = x[0].rearrange("(p j) n t -> p j (n t)", j=PACK)
         adj_tiles = []
-        x_sb = keep.tile([P, PACK, NODES * TIMES], BF16)
+        x_tiles = []
+        for g in range(PASSES):
+            x_sb = x_in.tile([P, PACK, BANK * TIMES], BF16, name="x_sb")
+            x_tiles.append(x_sb)
 
         def load_adj(r):
             adj_sb = adj_in.tile([P, NODES], BF16, name="adj_sb")
@@ -71,7 +75,7 @@ def tile_dynamicgraphspatialconv_pa_kernel(
         def load_x(g, u):
             cols = slice(g * BANK * TIMES, (g + 1) * BANK * TIMES)
             rows = slice(2 * u, 2 * u + 2)
-            nc.sync.dma_start(out=x_sb[:, rows, cols], in_=x_rows[:, rows, cols])
+            nc.sync.dma_start(out=x_tiles[g][:, rows, :], in_=x_rows[:, rows, cols])
 
         for r in range(3):
             load_adj(r)
@@ -120,12 +124,14 @@ def tile_dynamicgraphspatialconv_pa_kernel(
 
         x_by_c = keep.tile([P, TIMES, NODES, PACK], BF16, align_bytes=64)
 
-        x_by_t = x_sb[:].rearrange("p j (n t) -> p t j n", t=TIMES)
+        x_by_t = [x_sb[:].rearrange("p j (n t) -> p t j n", t=TIMES) for x_sb in x_tiles]
 
         def group_channels(i, t):
             nodes = slice(i * PIECE_NODES, (i + 1) * PIECE_NODES)
+            first = (i % 2) * PIECE_NODES
+            src = x_by_t[i // 2][:, t, :, first : first + PIECE_NODES].rearrange("p j n -> p n j")
             nc.gpsimd.tensor_scalar(
-                out=x_by_c[:, t, nodes, :], in0=x_by_t[:, t, :, nodes].rearrange("p j n -> p n j"),
+                out=x_by_c[:, t, nodes, :], in0=src,
                 scalar1=1.0, scalar2=0.0, op0=ALU.mult, op1=ALU.add,
             )
 
@@ -186,10 +192,13 @@ def tile_dynamicgraphspatialconv_pa_kernel(
             x_t = pool.tile([P, 2, PACK, P], BF16, name=tag)
             for jj in range(2):
                 for jn in range(PACK):
-                    first = (g * PACK + jn) * P
-                    nc.tensor.transpose(
-                        x_t[:, jj, jn, :], x_by_t[:, t, 2 * u + jj, first : first + P], ident_bf[:]
-                    )
+                    block = x_by_t[g][:, t, 2 * u + jj, jn * P : (jn + 1) * P]
+                    if (g, t, u) == (0, 0, 0):
+                        nc.tensor.transpose(x_t[:, jj, jn, :], block, ident_bf[:])
+                    else:
+                        nc.tensor.matmul(
+                            x_t[:, jj, jn, :], lhsT=block, rhs=ident_bf[:], start=True, stop=True
+                        )
             x_banks[g, t, u] = x_t
 
         def copy_x(g, t, u, engine="scalar"):

@@ -126,14 +126,20 @@ def tile_dynamicgraphspatialconv_pa_kernel(
 
         x_by_t = [x_sb[:].rearrange("p j (n t) -> p t j n", t=TIMES) for x_sb in x_tiles]
 
-        def group_channels(i, t):
-            nodes = slice(i * PIECE_NODES, (i + 1) * PIECE_NODES)
+        def group_channels(i, t, engine):
+            count = 1 if engine == "gpsimd" else 2
+            nodes = slice(i * PIECE_NODES, (i + count) * PIECE_NODES)
             first = (i % 2) * PIECE_NODES
-            src = x_by_t[i // 2][:, t, :, first : first + PIECE_NODES].rearrange("p j n -> p n j")
-            nc.gpsimd.tensor_scalar(
-                out=x_by_c[:, t, nodes, :], in0=src,
-                scalar1=1.0, scalar2=0.0, op0=ALU.mult, op1=ALU.add,
-            )
+            src = x_by_t[i // 2][:, t, :, first : first + count * PIECE_NODES].rearrange("p j n -> p n j")
+            if engine == "gpsimd":
+                nc.gpsimd.tensor_scalar(
+                    out=x_by_c[:, t, nodes, :], in0=src, scalar1=1.0, scalar2=0.0,
+                    op0=ALU.mult, op1=ALU.add,
+                )
+            elif engine == "vector":
+                nc.vector.tensor_copy(out=x_by_c[:, t, nodes, :], in_=src)
+            else:
+                nc.scalar.copy(out=x_by_c[:, t, nodes, :], in_=src)
 
         warm = keep.tile([P, 1], F32)
         nc.vector.memset(warm[:], 0.0)
@@ -163,17 +169,22 @@ def tile_dynamicgraphspatialconv_pa_kernel(
 
         junk = keep.tile([P, BANK], F32)
 
-        def sum_transposed(r):
-            sig_t = row_banks.tile([P, BANK], F32, name="r_row%d" % (r % 2))
+        def sum_transposed(r, pool, tag):
+            sig_t = pool.tile([P, BANK], F32, name=tag)
             for i in range(PACK):
                 nc.tensor.transpose(
                     sig_t[:, i * P : (i + 1) * P], sig[:, PACK + i, r * P : (r + 1) * P], ident[:]
                 )
+            sums_t[r] = sig_t
+
+        sums_t = {}
+
+        def sum_rest(r):
             nc.scalar.activation(
-                out=junk[:], in_=sig_t[:], func=ACT.Copy, accum_out=row_rest[:, r, 1:2]
+                out=junk[:], in_=sums_t[r][:], func=ACT.Copy, accum_out=row_rest[:, r, 1:2]
             )
 
-        def scale_rows(rows, first, width):
+        def scale_rows(rows, first, width, engine="vector"):
             cols = slice(first, first + width)
             for r in rows:
                 nc.vector.tensor_scalar(
@@ -193,7 +204,7 @@ def tile_dynamicgraphspatialconv_pa_kernel(
             for jj in range(2):
                 for jn in range(PACK):
                     block = x_by_t[g][:, t, 2 * u + jj, jn * P : (jn + 1) * P]
-                    if (g, t, u) == (0, 0, 0):
+                    if (g, u) == (0, 0):
                         nc.tensor.transpose(x_t[:, jj, jn, :], block, ident_bf[:])
                     else:
                         nc.tensor.matmul(
@@ -222,8 +233,8 @@ def tile_dynamicgraphspatialconv_pa_kernel(
         xc_words = keep.tile([P, TIMES, NODES], U32, align_bytes=64)
         xc_plane = keep.tile([P, TIMES, NODES], U8, align_bytes=64)
 
-        def quantise_channels(t, i):
-            nodes = slice(i * PIECE_NODES, (i + 1) * PIECE_NODES)
+        def quantise_channels(t, i, count=1):
+            nodes = slice(i * PIECE_NODES, (i + count) * PIECE_NODES)
             nc.vector.quantize_mx(
                 out=xc_words[:, t, nodes].bitcast(FP8X4),
                 scales=xc_plane[:, t, nodes],
@@ -261,7 +272,10 @@ def tile_dynamicgraphspatialconv_pa_kernel(
         def mirror(v, engine="scalar"):
             s_t = banks.tile([P, PACK, P], BF16, name="bank")
             for jn in range(PACK):
-                nc.tensor.transpose(s_t[:, jn, :], s_tiles[jn][:, 1, :, v - PACK], ident_bf[:])
+                nc.tensor.matmul(
+                    s_t[:, jn, :], lhsT=s_tiles[jn][:, 1, :, v - PACK], rhs=ident_bf[:],
+                    start=True, stop=True,
+                )
             dst, src = s_tiles[v][:, 0], s_t[:].rearrange("p jn q -> p q jn")
             if engine == "scalar":
                 nc.scalar.copy(out=dst, in_=src)
@@ -275,7 +289,7 @@ def tile_dynamicgraphspatialconv_pa_kernel(
                 in_=s_tiles[v][:].rearrange("p g q jn -> p (g q jn)"),
             )
 
-        def node_matmul(v, t):
+        def node_matmul(v, t, engine="scalar"):
             if t == 0:
                 tx_by_c = stage.tile([P, TIMES, P * PACK], BF16, name="tx_by_c", align_bytes=64)
                 tx_tiles[v] = tx_by_c
@@ -292,18 +306,22 @@ def tile_dynamicgraphspatialconv_pa_kernel(
                         start=(g == 0),
                         stop=(g == PASSES - 1),
                     )
-            nc.scalar.copy(
-                out=tx_by_c[:, t, :].rearrange("p (q j) -> p q j", j=PACK),
-                in_=tx[:].rearrange("p (j q) -> p q j", j=PACK),
-            )
+            dst = tx_by_c[:, t, :].rearrange("p (q j) -> p q j", j=PACK)
+            src = tx[:].rearrange("p (j q) -> p q j", j=PACK)
+            if engine == "scalar":
+                nc.scalar.copy(out=dst, in_=src)
+            else:
+                nc.vector.tensor_copy(out=dst, in_=src)
 
         def quantise_tx(v):
             tx_by_c = tx_tiles[v]
             tx_words = stage.tile([P, TIMES, P], U32, name="tx_words", align_bytes=64)
             tx_plane = stage.tile([P, TIMES, P], U8, name="tx_plane", align_bytes=64)
-            for t in range(TIMES):
+            for times in (slice(0, 2), slice(2, 3)):
                 nc.vector.quantize_mx(
-                    out=tx_words[:, t, :].bitcast(FP8X4), scales=tx_plane[:, t, :], in_=tx_by_c[:, t, :]
+                    out=tx_words[:, times, :].rearrange("p t q -> p (t q)").bitcast(FP8X4),
+                    scales=tx_plane[:, times, :].rearrange("p t q -> p (t q)"),
+                    in_=tx_by_c[:, times, :].rearrange("p t q -> p (t q)"),
                 )
             tx_tiles[v] = (tx_words, tx_plane)
 
@@ -335,33 +353,36 @@ def tile_dynamicgraphspatialconv_pa_kernel(
                 out=out[0, :, v * P : (v + 1) * P, :].rearrange("t q o -> q t o"), in_=result[:]
             )
 
-        for t in range(TIMES):
+        for t in range(2):
             turn_x(0, t, 0)
             copy_x(0, t, 0, "vector")
-            if t < 2:
-                for r in range(2):
-                    add_transposed(r, 2 * t, 2, t)
+            for r in range(2):
+                add_transposed(r, 2 * t, 2, t)
         for r in range(2, PACK):
             add_transposed(r, 0, PACK, 0)
-        for t in range(TIMES):
-            group_channels(0, t)
-        for r in range(PACK, CHUNKS):
-            if r >= 6:
-                sum_transposed(r - 6)
-            add_transposed(r, 0, PACK, 0)
-        for r in range(PACK, CHUNKS):
-            if r < 6:
-                sum_transposed(r - 2)
+        for i in range(2):
+            for t in range(TIMES):
+                group_channels(i, t, "gpsimd")
+        add_transposed(4, 0, PACK, 0)
+        add_transposed(5, 0, PACK, 0)
+        sum_transposed(0, row_banks, "r_row0")
+        add_transposed(6, 0, PACK, 0)
+        sum_transposed(1, row_banks, "r_row1")
+        add_transposed(7, 0, PACK, 0)
+        sum_transposed(2, out_banks, "acc")
+        add_transposed(4, PACK, PACK, 1)
+        sum_transposed(3, out_banks, "acc")
+        for r in range(5, CHUNKS):
             add_transposed(r, PACK, PACK, 1)
+        sum_rest(0)
+        sum_rest(1)
+        nc.scalar.activation(out=warm[:], in_=warm[:], func=ACT.Sqrt)
+        sum_rest(2)
+        sum_rest(3)
         turn_x(0, 0, 1)
         turn_x(1, 0, 0)
-        nc.scalar.activation(out=warm[:], in_=warm[:], func=ACT.Sqrt)
-        for i in range(1, PIECES):
-            for t in range(TIMES):
-                group_channels(i, t)
         turn_x(1, 0, 1, banks, "bank")
         turn_x(0, 1, 1, banks, "bank")
-        copy_x(0, 0, 1)
 
         deg = keep.tile([P, CHUNKS], F32)
         nc.vector.tensor_reduce(out=deg[:], in_=deg_parts[:], axis=AXIS.X, op=ALU.add)
@@ -370,7 +391,6 @@ def tile_dynamicgraphspatialconv_pa_kernel(
         nc.vector.tensor_tensor(out=deg[:, :PACK], in0=deg[:, :PACK], in1=rest[:], op=ALU.add)
         root = keep.tile([P, CHUNKS], F32)
         nc.scalar.activation(out=root[:], in_=deg[:], func=ACT.Sqrt)
-        quantise_nodes(0, 0)
         r_col = keep.tile([P, CHUNKS], F32)
         nc.vector.reciprocal(out=r_col[:], in_=root[:])
         for h in range(HALVES):
@@ -381,6 +401,7 @@ def tile_dynamicgraphspatialconv_pa_kernel(
                     r_row[:, i * P : (i + 1) * P], r_col[:, r : r + 1].to_broadcast([P, P]), ident[:]
                 )
             r_rows.append(r_row)
+        copy_x(0, 0, 1)
         copy_x(1, 0, 0)
         copy_x(1, 0, 1)
         copy_x(0, 1, 1)
@@ -388,54 +409,67 @@ def tile_dynamicgraphspatialconv_pa_kernel(
         turn_x(1, 1, 1)
         copy_x(1, 1, 0)
         copy_x(1, 1, 1)
-        scale_rows(range(CHUNKS), 0, P)
+        scale_rows(range(CHUNKS), 0, 2 * P)
         scale_columns(0)
-        quantise_nodes(1, 0)
+        quantise_nodes(0, 0)
         quantise_columns(0)
+        quantise_nodes(1, 0)
         node_matmul(0, 0)
-        scale_rows(range(CHUNKS), P, BANK - P)
         scale_columns(1)
         quantise_nodes(0, 1)
         quantise_columns(1)
+        turn_x(0, 2, 0)
+        copy_x(0, 2, 0)
         quantise_nodes(1, 1)
-        turn_x(0, 2, 1)
-        turn_x(1, 2, 0)
-        copy_x(0, 2, 1)
-        node_matmul(1, 0)
-        copy_x(1, 2, 0)
         node_matmul(0, 1)
+        node_matmul(1, 0)
+        turn_x(0, 2, 1)
+        copy_x(0, 2, 1)
+        node_matmul(1, 1)
+        turn_x(1, 2, 0)
+        copy_x(1, 2, 0)
+        scale_rows(range(CHUNKS), 2 * P, 2 * P)
+        scale_columns(2)
+        quantise_channels(0, 0, 2)
+        quantise_columns(2)
+        node_matmul(2, 0)
         turn_x(1, 2, 1)
         copy_x(1, 2, 1)
-        node_matmul(1, 1)
-        scale_columns(2)
-        quantise_nodes(0, 2)
-        quantise_columns(2)
-        quantise_nodes(1, 2)
+        node_matmul(2, 1)
         scale_columns(3)
-        for v in range(2):
-            node_matmul(v, 2)
-        quantise_channels(0, 0)
-        quantise_channels(1, 0)
+        quantise_nodes(0, 2)
         quantise_columns(3)
-        quantise_tx(0)
-        quantise_channels(2, 0)
+        quantise_channels(1, 0, 2)
+        quantise_nodes(1, 2)
+        for v in range(3):
+            node_matmul(v, 2)
         scale_rows(range(PACK, CHUNKS), BANK, BANK)
+        mirror(4)
+        mirror(5)
+        quantise_channels(2, 0, 2)
+        quantise_tx(0)
+        scale_columns(4)
+        quantise_tx(1)
+        quantise_columns(4)
 
-        for v in range(2, CHUNKS):
+        for v in range(3, CHUNKS):
             for t in range(TIMES):
                 node_matmul(v, t)
-            if v < 4:
-                mirror(2 * v)
-                mirror(2 * v + 1)
-            channel_matmuls(v - 2)
+            if v == 3:
+                mirror(6)
+                mirror(7)
+            channel_matmuls(v - 3)
+            if v == 7:
+                channel_matmuls(v - 2)
             if v + 2 < CHUNKS:
                 scale_columns(v + 2)
+            if v < 6:
+                group_channels(2, v - 3, "vector")
             quantise_tx(v - 1)
             if v + 2 < CHUNKS:
                 quantise_columns(v + 2)
-            if v < 5:
-                for t in range(TIMES):
-                    quantise_channels(t, v - 1)
+            if 3 < v < 7:
+                quantise_channels(v - 4, 2, 2)
         channel_matmuls(CHUNKS - 2)
         quantise_tx(CHUNKS - 1)
         channel_matmuls(CHUNKS - 1)

@@ -130,16 +130,19 @@ def tile_dynamicgraphspatialconv_pa_kernel(
             count = 1 if engine == "gpsimd" else 2
             nodes = slice(i * PIECE_NODES, (i + count) * PIECE_NODES)
             first = (i % 2) * PIECE_NODES
-            src = x_by_t[i // 2][:, t, :, first : first + count * PIECE_NODES].rearrange("p j n -> p n j")
+            src = x_by_t[i // 2][:, t, :, first : first + count * PIECE_NODES].rearrange(
+                "p j (b i) -> p b j i", i=4
+            )
+            dst = x_by_c[:, t, nodes, :].rearrange("p (b i) j -> p b j i", i=4)
             if engine == "gpsimd":
                 nc.gpsimd.tensor_scalar(
-                    out=x_by_c[:, t, nodes, :], in0=src, scalar1=1.0, scalar2=0.0,
+                    out=dst, in0=src, scalar1=1.0, scalar2=0.0,
                     op0=ALU.mult, op1=ALU.add,
                 )
             elif engine == "vector":
-                nc.vector.tensor_copy(out=x_by_c[:, t, nodes, :], in_=src)
+                nc.vector.tensor_copy(out=dst, in_=src)
             else:
-                nc.scalar.copy(out=x_by_c[:, t, nodes, :], in_=src)
+                nc.scalar.copy(out=dst, in_=src)
 
         warm = keep.tile([P, 1], F32)
         nc.vector.memset(warm[:], 0.0)
@@ -254,18 +257,13 @@ def tile_dynamicgraphspatialconv_pa_kernel(
             cols = slice(v * P, (v + 1) * P)
             s_by_n = s_tiles[v]
             row = r_rows[v // PACK][:, (v % PACK) * P : (v % PACK + 1) * P]
-            if v < PACK:
+            for g in range(PASSES) if v < PACK else (1,):
                 nc.vector.tensor_tensor(
-                    out=s_by_n[:],
-                    in0=a2[:, :, cols].rearrange("p (g jn) q -> p g q jn", g=PASSES),
-                    in1=row.unsqueeze(1).unsqueeze(3).to_broadcast([P, PASSES, P, PACK]),
-                    op=ALU.mult,
-                )
-            else:
-                nc.vector.tensor_tensor(
-                    out=s_by_n[:, 1],
-                    in0=a2[:, PACK:, cols].rearrange("p jn q -> p q jn"),
-                    in1=row.unsqueeze(2).to_broadcast([P, P, PACK]),
+                    out=s_by_n[:, g].rearrange("p (b i) jn -> p b jn i", i=4),
+                    in0=a2[:, g * PACK : (g + 1) * PACK, cols].rearrange("p jn (b i) -> p b jn i", i=4),
+                    in1=row.rearrange("p (b i) -> p b i", i=4)
+                    .unsqueeze(2)
+                    .to_broadcast([P, P // 4, PACK, 4]),
                     op=ALU.mult,
                 )
 

@@ -69,21 +69,25 @@ def tile_dynamicgraphspatialconv_pa_kernel(
 
         def load_adj(r):
             adj_sb = adj_in.tile([P, NODES], BF16, name="adj_sb")
-            nc.sync.dma_start(out=adj_sb[:], in_=adj_param[r * P : (r + 1) * P, :])
+            for cols in (slice(0, BANK), slice(BANK, NODES)) if r == 0 else (slice(0, NODES),):
+                nc.sync.dma_start(out=adj_sb[:, cols], in_=adj_param[r * P : (r + 1) * P, cols])
             adj_tiles.append(adj_sb)
 
-        def load_x(g, u):
+        def load_x(g, first, last):
             cols = slice(g * BANK * TIMES, (g + 1) * BANK * TIMES)
-            rows = slice(2 * u, 2 * u + 2)
+            rows = slice(first, last)
             nc.sync.dma_start(out=x_tiles[g][:, rows, :], in_=x_rows[:, rows, cols])
 
-        for r in range(3):
+        for r in range(2):
             load_adj(r)
-        load_x(0, 0)
+        load_x(0, 0, 1)
+        load_adj(2)
+        load_x(0, 1, 2)
         for r in range(3, CHUNKS):
             load_adj(r)
-        for g, u in ((0, 1), (1, 0), (1, 1)):
-            load_x(g, u)
+        load_x(0, 2, 4)
+        load_x(1, 0, 2)
+        load_x(1, 2, 4)
         for words, plane, words_in, scales_in in weights:
             nc.sync.dma_start(
                 out=words[:].bitcast(I32),
@@ -130,16 +134,17 @@ def tile_dynamicgraphspatialconv_pa_kernel(
             count = 1 if engine == "gpsimd" else 2
             nodes = slice(i * PIECE_NODES, (i + count) * PIECE_NODES)
             first = (i % 2) * PIECE_NODES
-            src = x_by_t[i // 2][:, t, :, first : first + count * PIECE_NODES].rearrange(
-                "p j (b i) -> p b j i", i=4
-            )
-            dst = x_by_c[:, t, nodes, :].rearrange("p (b i) j -> p b j i", i=4)
+            src = x_by_t[i // 2][:, t, :, first : first + count * PIECE_NODES]
+            dst = x_by_c[:, t, nodes, :]
             if engine == "gpsimd":
                 nc.gpsimd.tensor_scalar(
-                    out=dst, in0=src, scalar1=1.0, scalar2=0.0,
+                    out=dst, in0=src.rearrange("p j n -> p n j"), scalar1=1.0, scalar2=0.0,
                     op0=ALU.mult, op1=ALU.add,
                 )
-            elif engine == "vector":
+                return
+            src = src.rearrange("p j (b i) -> p b j i", i=4)
+            dst = dst.rearrange("p (b i) j -> p b j i", i=4)
+            if engine == "vector":
                 nc.vector.tensor_copy(out=dst, in_=src)
             else:
                 nc.scalar.copy(out=dst, in_=src)
@@ -202,25 +207,20 @@ def tile_dynamicgraphspatialconv_pa_kernel(
 
         x_banks = {}
 
-        def turn_x(g, t, u, pool=out_banks, tag="acc"):
-            x_t = pool.tile([P, 2, PACK, P], BF16, name=tag)
-            for jj in range(2):
+        def turn_x(g, t, first, last, pool=out_banks, tag="acc"):
+            x_t = pool.tile([P, last - first, PACK, P], BF16, name=tag)
+            for j in range(first, last):
                 for jn in range(PACK):
-                    block = x_by_t[g][:, t, 2 * u + jj, jn * P : (jn + 1) * P]
-                    if (g, u) == (0, 0):
-                        nc.tensor.transpose(x_t[:, jj, jn, :], block, ident_bf[:])
-                    else:
-                        nc.tensor.matmul(
-                            x_t[:, jj, jn, :], lhsT=block, rhs=ident_bf[:], start=True, stop=True
-                        )
-            x_banks[g, t, u] = x_t
+                    block = x_by_t[g][:, t, j, jn * P : (jn + 1) * P]
+                    nc.tensor.transpose(x_t[:, j - first, jn, :], block, ident_bf[:])
+            x_banks[g, t, first] = x_t[:].rearrange("p j jn m -> p j m jn")
 
-        def copy_x(g, t, u, engine="scalar"):
+        def copy_x(g, t, first, last, engine="scalar"):
             if (g, t) not in x_by_n_tiles:
                 x_by_n = x_stage.tile([P, PACK, P, PACK], BF16, name="x_by_n", align_bytes=64)
                 x_by_n_tiles[g, t] = x_by_n
-            dst = x_by_n_tiles[g, t][:, 2 * u : 2 * u + 2]
-            src = x_banks[g, t, u][:].rearrange("p jj jn m -> p jj m jn")
+            dst = x_by_n_tiles[g, t][:, first:last]
+            src = x_banks[g, t, first]
             if engine == "scalar":
                 nc.scalar.copy(out=dst, in_=src)
             else:
@@ -270,10 +270,7 @@ def tile_dynamicgraphspatialconv_pa_kernel(
         def mirror(v, engine="scalar"):
             s_t = banks.tile([P, PACK, P], BF16, name="bank")
             for jn in range(PACK):
-                nc.tensor.matmul(
-                    s_t[:, jn, :], lhsT=s_tiles[jn][:, 1, :, v - PACK], rhs=ident_bf[:],
-                    start=True, stop=True,
-                )
+                nc.tensor.transpose(s_t[:, jn, :], s_tiles[jn][:, 1, :, v - PACK], ident_bf[:])
             dst, src = s_tiles[v][:, 0], s_t[:].rearrange("p jn q -> p q jn")
             if engine == "scalar":
                 nc.scalar.copy(out=dst, in_=src)
@@ -323,9 +320,9 @@ def tile_dynamicgraphspatialconv_pa_kernel(
                 )
             tx_tiles[v] = (tx_words, tx_plane)
 
-        def channel_matmuls(v):
+        def channel_matmuls(v, parts=((0, TIMES, "scalar"),), pool=out_banks, tag="acc"):
             tx_words, tx_plane = tx_tiles[v]
-            acc = out_banks.tile([P, TIMES, OUTS], F32, name="acc")
+            acc = pool.tile([P, TIMES, OUTS], F32, name=tag)
             for t in range(TIMES):
                 nc.tensor.matmul_mx(
                     out=acc[:, t, :],
@@ -346,41 +343,50 @@ def tile_dynamicgraphspatialconv_pa_kernel(
                     stop=True,
                 )
             result = stage.tile([P, TIMES, OUTS], F32, name="result")
-            nc.scalar.copy(out=result[:], in_=acc[:])
-            nc.sync.dma_start(
-                out=out[0, :, v * P : (v + 1) * P, :].rearrange("t q o -> q t o"), in_=result[:]
-            )
+            for first, last, engine in parts:
+                if engine == "scalar":
+                    nc.scalar.copy(out=result[:, first:last], in_=acc[:, first:last])
+                else:
+                    nc.vector.tensor_copy(out=result[:, first:last], in_=acc[:, first:last])
+                nc.sync.dma_start(
+                    out=out[0, first:last, v * P : (v + 1) * P, :].rearrange("t q o -> q t o"),
+                    in_=result[:, first:last],
+                )
 
-        for t in range(2):
-            turn_x(0, t, 0)
-            copy_x(0, t, 0, "vector")
-            for r in range(2):
-                add_transposed(r, 2 * t, 2, t)
+        for t in range(TIMES):
+            turn_x(0, t, 0, 1)
+            copy_x(0, t, 0, 1, "vector")
+        for r in range(2):
+            add_transposed(r, 0, 2, 0)
+        for t in range(TIMES):
+            turn_x(0, t, 1, 2)
+            copy_x(0, t, 1, 2, "vector")
+        for r in range(2):
+            add_transposed(r, 2, 2, 1)
         for r in range(2, PACK):
             add_transposed(r, 0, PACK, 0)
-        for i in range(2):
+        for i in range(PIECES):
             for t in range(TIMES):
                 group_channels(i, t, "gpsimd")
         add_transposed(4, 0, PACK, 0)
         add_transposed(5, 0, PACK, 0)
-        sum_transposed(0, row_banks, "r_row0")
         add_transposed(6, 0, PACK, 0)
-        sum_transposed(1, row_banks, "r_row1")
-        add_transposed(7, 0, PACK, 0)
-        sum_transposed(2, out_banks, "acc")
-        add_transposed(4, PACK, PACK, 1)
-        sum_transposed(3, out_banks, "acc")
-        for r in range(5, CHUNKS):
-            add_transposed(r, PACK, PACK, 1)
+        sum_transposed(0, row_banks, "r_row0")
         sum_rest(0)
+        add_transposed(7, 0, PACK, 0)
+        sum_transposed(1, row_banks, "r_row1")
         sum_rest(1)
         nc.scalar.activation(out=warm[:], in_=warm[:], func=ACT.Sqrt)
+        add_transposed(4, PACK, PACK, 1)
+        add_transposed(5, PACK, PACK, 1)
+        sum_transposed(2, row_banks, "r_row0")
+        add_transposed(6, PACK, PACK, 1)
+        sum_transposed(3, row_banks, "r_row1")
+        add_transposed(7, PACK, PACK, 1)
         sum_rest(2)
         sum_rest(3)
-        turn_x(0, 0, 1)
-        turn_x(1, 0, 0)
-        turn_x(1, 0, 1, banks, "bank")
-        turn_x(0, 1, 1, banks, "bank")
+        turn_x(0, 0, 2, 4, pool=banks, tag="bank")
+        turn_x(1, 0, 0, 2)
 
         deg = keep.tile([P, CHUNKS], F32)
         nc.vector.tensor_reduce(out=deg[:], in_=deg_parts[:], axis=AXIS.X, op=ALU.add)
@@ -399,14 +405,16 @@ def tile_dynamicgraphspatialconv_pa_kernel(
                     r_row[:, i * P : (i + 1) * P], r_col[:, r : r + 1].to_broadcast([P, P]), ident[:]
                 )
             r_rows.append(r_row)
-        copy_x(0, 0, 1)
-        copy_x(1, 0, 0)
-        copy_x(1, 0, 1)
-        copy_x(0, 1, 1)
-        turn_x(1, 1, 0)
-        turn_x(1, 1, 1)
-        copy_x(1, 1, 0)
-        copy_x(1, 1, 1)
+        turn_x(1, 0, 2, 4)
+        turn_x(0, 1, 2, 4, pool=banks, tag="bank")
+        copy_x(0, 0, 2, 4)
+        copy_x(1, 0, 0, 2)
+        copy_x(1, 0, 2, 4)
+        copy_x(0, 1, 2, 4)
+        turn_x(1, 1, 0, 2)
+        turn_x(1, 1, 2, 4)
+        copy_x(1, 1, 0, 2)
+        copy_x(1, 1, 2, 4)
         scale_rows(range(CHUNKS), 0, 2 * P)
         scale_columns(0)
         quantise_nodes(0, 0)
@@ -416,29 +424,27 @@ def tile_dynamicgraphspatialconv_pa_kernel(
         scale_columns(1)
         quantise_nodes(0, 1)
         quantise_columns(1)
-        turn_x(0, 2, 0)
-        copy_x(0, 2, 0)
+        turn_x(0, 2, 2, 4)
+        copy_x(0, 2, 2, 4)
+        node_matmul(1, 0)
         quantise_nodes(1, 1)
         node_matmul(0, 1)
-        node_matmul(1, 0)
-        turn_x(0, 2, 1)
-        copy_x(0, 2, 1)
+        turn_x(1, 2, 0, 2)
+        copy_x(1, 2, 0, 2)
         node_matmul(1, 1)
-        turn_x(1, 2, 0)
-        copy_x(1, 2, 0)
+        turn_x(1, 2, 2, 4)
+        copy_x(1, 2, 2, 4)
         scale_rows(range(CHUNKS), 2 * P, 2 * P)
         scale_columns(2)
         quantise_channels(0, 0, 2)
         quantise_columns(2)
         node_matmul(2, 0)
-        turn_x(1, 2, 1)
-        copy_x(1, 2, 1)
         node_matmul(2, 1)
-        scale_columns(3)
         quantise_nodes(0, 2)
-        quantise_columns(3)
-        quantise_channels(1, 0, 2)
         quantise_nodes(1, 2)
+        scale_columns(3)
+        quantise_channels(1, 0, 2)
+        quantise_columns(3)
         for v in range(3):
             node_matmul(v, 2)
         scale_rows(range(PACK, CHUNKS), BANK, BANK)
@@ -456,18 +462,24 @@ def tile_dynamicgraphspatialconv_pa_kernel(
             if v == 3:
                 mirror(6)
                 mirror(7)
-            channel_matmuls(v - 3)
-            if v == 7:
-                channel_matmuls(v - 2)
-            if v + 2 < CHUNKS:
-                scale_columns(v + 2)
             if v < 6:
-                group_channels(2, v - 3, "vector")
+                channel_matmuls(v - 3)
+            if v < 5:
+                scale_columns(v + 2)
+            if v == 4:
+                scale_columns(7)
             quantise_tx(v - 1)
-            if v + 2 < CHUNKS:
+            if v < 5:
                 quantise_columns(v + 2)
-            if 3 < v < 7:
-                quantise_channels(v - 4, 2, 2)
-        channel_matmuls(CHUNKS - 2)
+            if v == 4:
+                quantise_columns(7)
+            if v == 5:
+                quantise_channels(0, 2, 2)
+                quantise_channels(1, 2, 2)
+                quantise_channels(2, 2, 2)
+            if v >= 6:
+                channel_matmuls(v - 3, ((0, TIMES, "vector"),))
+        channel_matmuls(CHUNKS - 3, ((0, TIMES, "scalar"),), banks, "bank")
         quantise_tx(CHUNKS - 1)
-        channel_matmuls(CHUNKS - 1)
+        channel_matmuls(CHUNKS - 2, ((0, TIMES, "scalar"),), banks, "bank")
+        channel_matmuls(CHUNKS - 1, ((0, 2, "scalar"), (2, TIMES, "vector")), banks, "bank")

@@ -212,19 +212,26 @@ def tile_dynamicgraphspatialconv_pa_kernel(
             for j in range(first, last):
                 for jn in range(PACK):
                     block = x_by_t[g][:, t, j, jn * P : (jn + 1) * P]
-                    nc.tensor.transpose(x_t[:, j - first, jn, :], block, ident_bf[:])
-            x_banks[g, t, first] = x_t[:].rearrange("p j jn m -> p j m jn")
+                    if last - first == 1:
+                        nc.tensor.transpose(x_t[:, j - first, jn, :], block, ident_bf[:])
+                    else:
+                        nc.tensor.matmul(
+                            x_t[:, j - first, jn, :], lhsT=block, rhs=ident_bf[:],
+                            start=True, stop=True,
+                        )
+            x_banks[g, t, first] = x_t
 
         def copy_x(g, t, first, last, engine="scalar"):
             if (g, t) not in x_by_n_tiles:
                 x_by_n = x_stage.tile([P, PACK, P, PACK], BF16, name="x_by_n", align_bytes=64)
                 x_by_n_tiles[g, t] = x_by_n
-            dst = x_by_n_tiles[g, t][:, first:last]
-            src = x_banks[g, t, first]
-            if engine == "scalar":
-                nc.scalar.copy(out=dst, in_=src)
-            else:
-                nc.vector.tensor_copy(out=dst, in_=src)
+            for j in range(first, last):
+                dst = x_by_n_tiles[g, t][:, j].rearrange("p (b i) jn -> p b jn i", i=4)
+                src = x_banks[g, t, first][:, j - first].rearrange("p jn (b i) -> p b jn i", i=4)
+                if engine == "scalar":
+                    nc.scalar.copy(out=dst, in_=src)
+                else:
+                    nc.vector.tensor_copy(out=dst, in_=src)
 
         def quantise_nodes(g, t):
             nc.vector.quantize_mx(
@@ -270,8 +277,12 @@ def tile_dynamicgraphspatialconv_pa_kernel(
         def mirror(v, engine="scalar"):
             s_t = banks.tile([P, PACK, P], BF16, name="bank")
             for jn in range(PACK):
-                nc.tensor.transpose(s_t[:, jn, :], s_tiles[jn][:, 1, :, v - PACK], ident_bf[:])
-            dst, src = s_tiles[v][:, 0], s_t[:].rearrange("p jn q -> p q jn")
+                nc.tensor.matmul(
+                    s_t[:, jn, :], lhsT=s_tiles[jn][:, 1, :, v - PACK], rhs=ident_bf[:],
+                    start=True, stop=True,
+                )
+            dst = s_tiles[v][:, 0].rearrange("p (b i) jn -> p b jn i", i=4)
+            src = s_t[:].rearrange("p jn (b i) -> p b jn i", i=4)
             if engine == "scalar":
                 nc.scalar.copy(out=dst, in_=src)
             else:
@@ -301,8 +312,8 @@ def tile_dynamicgraphspatialconv_pa_kernel(
                         start=(g == 0),
                         stop=(g == PASSES - 1),
                     )
-            dst = tx_by_c[:, t, :].rearrange("p (q j) -> p q j", j=PACK)
-            src = tx[:].rearrange("p (j q) -> p q j", j=PACK)
+            dst = tx_by_c[:, t, :].rearrange("p (b i j) -> p b j i", j=PACK, i=4)
+            src = tx[:].rearrange("p (j b i) -> p b j i", j=PACK, i=4)
             if engine == "scalar":
                 nc.scalar.copy(out=dst, in_=src)
             else:
@@ -365,10 +376,10 @@ def tile_dynamicgraphspatialconv_pa_kernel(
             add_transposed(r, 2, 2, 1)
         for r in range(2, PACK):
             add_transposed(r, 0, PACK, 0)
-        for i in range(PIECES):
-            for t in range(TIMES):
-                group_channels(i, t, "gpsimd")
+        for i, t in ((0, 1), (1, 1), (0, 2), (1, 2), (2, 0), (3, 0)):
+            group_channels(i, t, "gpsimd")
         add_transposed(4, 0, PACK, 0)
+        group_channels(0, 0, "vector")
         add_transposed(5, 0, PACK, 0)
         add_transposed(6, 0, PACK, 0)
         sum_transposed(0, row_banks, "r_row0")
@@ -462,8 +473,7 @@ def tile_dynamicgraphspatialconv_pa_kernel(
             if v == 3:
                 mirror(6)
                 mirror(7)
-            if v < 6:
-                channel_matmuls(v - 3)
+            channel_matmuls(v - 3)
             if v < 5:
                 scale_columns(v + 2)
             if v == 4:
@@ -474,11 +484,11 @@ def tile_dynamicgraphspatialconv_pa_kernel(
             if v == 4:
                 quantise_columns(7)
             if v == 5:
+                group_channels(2, 1, "vector")
                 quantise_channels(0, 2, 2)
+                group_channels(2, 2, "vector")
                 quantise_channels(1, 2, 2)
                 quantise_channels(2, 2, 2)
-            if v >= 6:
-                channel_matmuls(v - 3, ((0, TIMES, "vector"),))
         channel_matmuls(CHUNKS - 3, ((0, TIMES, "scalar"),), banks, "bank")
         quantise_tx(CHUNKS - 1)
         channel_matmuls(CHUNKS - 2, ((0, TIMES, "scalar"),), banks, "bank")

@@ -219,19 +219,18 @@ def tile_dynamicgraphspatialconv_pa_kernel(
                             x_t[:, j - first, jn, :], lhsT=block, rhs=ident_bf[:],
                             start=True, stop=True,
                         )
-            x_banks[g, t, first] = x_t
+            x_banks[g, t, first] = x_t[:].rearrange("p j jn m -> p j m jn")
 
         def copy_x(g, t, first, last, engine="scalar"):
             if (g, t) not in x_by_n_tiles:
                 x_by_n = x_stage.tile([P, PACK, P, PACK], BF16, name="x_by_n", align_bytes=64)
                 x_by_n_tiles[g, t] = x_by_n
-            for j in range(first, last):
-                dst = x_by_n_tiles[g, t][:, j].rearrange("p (b i) jn -> p b jn i", i=4)
-                src = x_banks[g, t, first][:, j - first].rearrange("p jn (b i) -> p b jn i", i=4)
-                if engine == "scalar":
-                    nc.scalar.copy(out=dst, in_=src)
-                else:
-                    nc.vector.tensor_copy(out=dst, in_=src)
+            dst = x_by_n_tiles[g, t][:, first:last]
+            src = x_banks[g, t, first]
+            if engine == "scalar":
+                nc.scalar.copy(out=dst, in_=src)
+            else:
+                nc.vector.tensor_copy(out=dst, in_=src)
 
         def quantise_nodes(g, t):
             nc.vector.quantize_mx(
@@ -281,8 +280,7 @@ def tile_dynamicgraphspatialconv_pa_kernel(
                     s_t[:, jn, :], lhsT=s_tiles[jn][:, 1, :, v - PACK], rhs=ident_bf[:],
                     start=True, stop=True,
                 )
-            dst = s_tiles[v][:, 0].rearrange("p (b i) jn -> p b jn i", i=4)
-            src = s_t[:].rearrange("p jn (b i) -> p b jn i", i=4)
+            dst, src = s_tiles[v][:, 0], s_t[:].rearrange("p jn q -> p q jn")
             if engine == "scalar":
                 nc.scalar.copy(out=dst, in_=src)
             else:
@@ -312,8 +310,8 @@ def tile_dynamicgraphspatialconv_pa_kernel(
                         start=(g == 0),
                         stop=(g == PASSES - 1),
                     )
-            dst = tx_by_c[:, t, :].rearrange("p (b i j) -> p b j i", j=PACK, i=4)
-            src = tx[:].rearrange("p (j b i) -> p b j i", j=PACK, i=4)
+            dst = tx_by_c[:, t, :].rearrange("p (q j) -> p q j", j=PACK)
+            src = tx[:].rearrange("p (j q) -> p q j", j=PACK)
             if engine == "scalar":
                 nc.scalar.copy(out=dst, in_=src)
             else:
@@ -364,17 +362,14 @@ def tile_dynamicgraphspatialconv_pa_kernel(
                     in_=result[:, first:last],
                 )
 
-        for t in range(TIMES):
-            turn_x(0, t, 0, 1)
-            copy_x(0, t, 0, 1, "vector")
-        for r in range(2):
-            add_transposed(r, 0, 2, 0)
-        for t in range(TIMES):
-            turn_x(0, t, 1, 2)
-            copy_x(0, t, 1, 2, "vector")
-        for r in range(2):
-            add_transposed(r, 2, 2, 1)
-        for r in range(2, PACK):
+        for j in range(2):
+            for t in range(TIMES):
+                if t == 1:
+                    turn_x(0, t, j, j + 1, banks, "bank")
+                else:
+                    turn_x(0, t, j, j + 1)
+                copy_x(0, t, j, j + 1, "vector")
+        for r in range(PACK):
             add_transposed(r, 0, PACK, 0)
         for i, t in ((0, 1), (1, 1), (0, 2), (1, 2), (2, 0), (3, 0)):
             group_channels(i, t, "gpsimd")

@@ -376,6 +376,8 @@ def tile_dynamicgraphspatialconv_pa_kernel(
         add_transposed(4, 0, PACK, 0)
         group_channels(0, 0, "vector")
         add_transposed(5, 0, PACK, 0)
+        turn_x(0, 0, 2, 4)
+        copy_x(0, 0, 2, 4)
         add_transposed(6, 0, PACK, 0)
         sum_transposed(0, row_banks, "r_row0")
         sum_rest(0)
@@ -391,8 +393,9 @@ def tile_dynamicgraphspatialconv_pa_kernel(
         add_transposed(7, PACK, PACK, 1)
         sum_rest(2)
         sum_rest(3)
-        turn_x(0, 0, 2, 4, pool=banks, tag="bank")
         turn_x(1, 0, 0, 2)
+        turn_x(1, 0, 2, 4)
+        turn_x(0, 1, 2, 4, pool=banks, tag="bank")
 
         deg = keep.tile([P, CHUNKS], F32)
         nc.vector.tensor_reduce(out=deg[:], in_=deg_parts[:], axis=AXIS.X, op=ALU.add)
@@ -411,9 +414,6 @@ def tile_dynamicgraphspatialconv_pa_kernel(
                     r_row[:, i * P : (i + 1) * P], r_col[:, r : r + 1].to_broadcast([P, P]), ident[:]
                 )
             r_rows.append(r_row)
-        turn_x(1, 0, 2, 4)
-        turn_x(0, 1, 2, 4, pool=banks, tag="bank")
-        copy_x(0, 0, 2, 4)
         copy_x(1, 0, 0, 2)
         copy_x(1, 0, 2, 4)
         copy_x(0, 1, 2, 4)
@@ -431,15 +431,15 @@ def tile_dynamicgraphspatialconv_pa_kernel(
         quantise_nodes(0, 1)
         quantise_columns(1)
         turn_x(0, 2, 2, 4)
+        turn_x(1, 2, 0, 2)
         copy_x(0, 2, 2, 4)
+        copy_x(1, 2, 0, 2)
         node_matmul(1, 0)
         quantise_nodes(1, 1)
         node_matmul(0, 1)
-        turn_x(1, 2, 0, 2)
-        copy_x(1, 2, 0, 2)
-        node_matmul(1, 1)
         turn_x(1, 2, 2, 4)
         copy_x(1, 2, 2, 4)
+        node_matmul(1, 1)
         scale_rows(range(CHUNKS), 2 * P, 2 * P)
         scale_columns(2)
         quantise_channels(0, 0, 2)

import concourse.mybir as mybir
from concourse.masks import make_identity

F32 = mybir.dt.float32
BF16 = mybir.dt.bfloat16
U32 = mybir.dt.uint32
U8 = mybir.dt.uint8
I32 = mybir.dt.int32
FP8X4 = mybir.dt.float8_e4m3fn_x4
ACT = mybir.ActivationFunctionType
ALU = mybir.AluOpType
AXIS = mybir.AxisListType

P = 128
PACK = 4
NODES = 1024
CHANNELS = 512
TIMES = 3
OUTS = 128
CHUNKS = NODES // P
PASSES = NODES // (P * PACK)
BANK = 512
HALVES = NODES // BANK
PIECES = 4
PIECE_NODES = NODES // PIECES
AHEAD = 3
LAG = 2

FLOPS = 2 * TIMES * NODES * (NODES * CHANNELS + 2 * CHANNELS * OUTS)


def tile_dynamicgraphspatialconv_pa_kernel(
    tc, x, adj_param, w_cheb0_words, w_cheb0_scales, w_cheb1_words, w_cheb1_scales, out
):
    nc = tc.nc
    with (
        tc.tile_pool(name="keep", bufs=1) as keep,
        tc.tile_pool(name="adj_in", bufs=CHUNKS) as adj_in,
        tc.tile_pool(name="stage", bufs=4) as stage,
        tc.tile_pool(name="x_in", bufs=PASSES) as x_in,
        tc.tile_pool(name="x_stage", bufs=6) as x_stage,
        tc.tile_pool(name="s_stage", bufs=CHUNKS) as s_stage,
        tc.psum_pool(name="banks", bufs=4) as banks,
        tc.psum_pool(name="row_banks", bufs=1) as row_banks,
        tc.psum_pool(name="out_banks", bufs=2) as out_banks,
        tc.manual_schedule(),
    ):
        ident = keep.tile([P, P], F32)
        make_identity(nc, ident[:])
        ident_bf = keep.tile([P, P], BF16)
        make_identity(nc, ident_bf[:])

        weights = []
        for name, words_in, scales_in in (
            ("w0", w_cheb0_words, w_cheb0_scales),
            ("w1", w_cheb1_words, w_cheb1_scales),
        ):
            words = keep.tile([P, OUTS], U32, name=name + "_words", align_bytes=64)
            plane = keep.tile([P, OUTS], U8, name=name + "_plane", align_bytes=64)
            nc.vector.memset(plane[:].bitcast(I32), 0)
            weights.append((words, plane, words_in, scales_in))

        x_rows = x[0].rearrange("(p j) n t -> p j (n t)", j=PACK)
        adj_tiles = []
        x_tiles = []
        for g in range(PASSES):
            x_sb = x_in.tile([P, PACK, BANK * TIMES], BF16, name="x_sb")
            x_tiles.append(x_sb)

        def load_adj(r):
            adj_sb = adj_in.tile([P, NODES], BF16, name="adj_sb")
            for cols in (slice(0, BANK), slice(BANK, NODES)) if r == 0 else (slice(0, NODES),):
                nc.sync.dma_start(out=adj_sb[:, cols], in_=adj_param[r * P : (r + 1) * P, cols])
            adj_tiles.append(adj_sb)

        def load_x(g, first, last):
            cols = slice(g * BANK * TIMES, (g + 1) * BANK * TIMES)
            rows = slice(first, last)
            nc.sync.dma_start(out=x_tiles[g][:, rows, :], in_=x_rows[:, rows, cols])

        for r in range(2):
            load_adj(r)
        load_x(0, 0, 1)
        load_adj(2)
        load_x(0, 1, 2)
        for r in range(3, CHUNKS):
            load_adj(r)
        load_x(0, 2, 4)
        load_x(1, 0, 2)
        load_x(1, 2, 4)
        for words, plane, words_in, scales_in in weights:
            nc.sync.dma_start(
                out=words[:].bitcast(I32),
                in_=words_in[0].rearrange("p n t -> p (n t)").bitcast(I32),
            )
            for q in range(4):
                nc.sync.dma_start(
                    out=plane[32 * q : 32 * q + 4, :].bitcast(I32),
                    in_=scales_in[0, 4 * q : 4 * q + 4, :].bitcast(I32),
                )

        sig = keep.tile([P, CHUNKS, NODES], F32)

        def mask_diagonal(r):
            source, fill = (sig[:, r, :], 0.0) if r == 0 else (adj_tiles[r], -512.0)
            diag = source[:, r * P : (r + 1) * P]
            nc.gpsimd.affine_select(
                out=diag,
                in_=diag,
                pattern=[[-1, P]],
                compare_op=ALU.not_equal,
                fill=fill,
                base=0,
                channel_multiplier=1,
            )

        row_rest = keep.tile([P, PACK, 2], F32)

        def sigmoid_chunk(r):
            if r >= PACK:
                nc.scalar.activation(out=sig[:, r, :], in_=adj_tiles[r][:], func=ACT.Sigmoid)
                return
            nc.scalar.activation(out=sig[:, r, :BANK], in_=adj_tiles[r][:, :BANK], func=ACT.Sigmoid)
            nc.scalar.activation(
                out=sig[:, r, BANK:], in_=adj_tiles[r][:, BANK:], func=ACT.Sigmoid,
                accum_out=row_rest[:, r, 0:1],
            )

        x_by_c = keep.tile([P, TIMES, NODES, PACK], BF16, align_bytes=64)

        x_by_t = [x_sb[:].rearrange("p j (n t) -> p t j n", t=TIMES) for x_sb in x_tiles]

        def group_channels(i, t, engine):
            count = 1 if engine == "gpsimd" else 2
            nodes = slice(i * PIECE_NODES, (i + count) * PIECE_NODES)
            first = (i % 2) * PIECE_NODES
            src = x_by_t[i // 2][:, t, :, first : first + count * PIECE_NODES]
            dst = x_by_c[:, t, nodes, :]
            if engine == "gpsimd":
                nc.gpsimd.tensor_scalar(
                    out=dst, in0=src.rearrange("p j n -> p n j"), scalar1=1.0, scalar2=0.0,
                    op0=ALU.mult, op1=ALU.add,
                )
                return
            src = src.rearrange("p j (b i) -> p b j i", i=4)
            dst = dst.rearrange("p (b i) j -> p b j i", i=4)
            if engine == "vector":
                nc.vector.tensor_copy(out=dst, in_=src)
            else:
                nc.scalar.copy(out=dst, in_=src)

        warm = keep.tile([P, 1], F32)
        nc.vector.memset(warm[:], 0.0)
        nc.scalar.activation(out=warm[:], in_=warm[:], func=ACT.Sigmoid)
        for r in range(1, CHUNKS):
            mask_diagonal(r)
            if r == 1:
                sigmoid_chunk(0)
            if r == 2:
                mask_diagonal(0)
            sigmoid_chunk(r)
        a2 = keep.tile([P, CHUNKS, NODES], F32)
        deg_parts = keep.tile([P, CHUNKS, HALVES], F32)
        nc.vector.memset(deg_parts[:], 0.0)

        def add_transposed(r, first, count, part):
            sig_t = banks.tile([P, BANK], F32, name="bank")
            for i in range(count):
                nc.tensor.transpose(
                    sig_t[:, i * P : (i + 1) * P], sig[:, first + i, r * P : (r + 1) * P], ident[:]
                )
            cols = slice(first * P, (first + count) * P)
            nc.vector.scalar_tensor_tensor(
                out=a2[:, r, cols], in0=sig[:, r, cols], scalar=1.0, in1=sig_t[:, : count * P],
                op0=ALU.mult, op1=ALU.add, accum_out=deg_parts[:, r, part : part + 1],
            )

        junk = keep.tile([P, BANK], F32)

        def sum_transposed(r, pool, tag):
            sig_t = pool.tile([P, BANK], F32, name=tag)
            for i in range(PACK):
                nc.tensor.transpose(
                    sig_t[:, i * P : (i + 1) * P], sig[:, PACK + i, r * P : (r + 1) * P], ident[:]
                )
            sums_t[r] = sig_t

        sums_t = {}

        def sum_rest(r):
            nc.scalar.activation(
                out=junk[:], in_=sums_t[r][:], func=ACT.Copy, accum_out=row_rest[:, r, 1:2]
            )

        def scale_rows(rows, first, width, engine="vector"):
            cols = slice(first, first + width)
            for r in rows:
                nc.vector.tensor_scalar(
                    out=a2[:, r, cols], in0=a2[:, r, cols], scalar1=r_col[:, r : r + 1],
                    scalar2=-1.0, op0=ALU.mult, op1=ALU.mult,
                )

        xn_words = keep.tile([P, TIMES, PASSES, CHANNELS], U32, align_bytes=64)
        xn_plane = keep.tile([P, TIMES, PASSES, CHANNELS], U8, align_bytes=64)

        x_by_n_tiles = {}

        x_banks = {}

        def turn_x(g, t, first, last, pool=out_banks, tag="acc"):
            x_t = pool.tile([P, last - first, PACK, P], BF16, name=tag)
            for j in range(first, last):
                for jn in range(PACK):
                    block = x_by_t[g][:, t, j, jn * P : (jn + 1) * P]
                    if last - first == 1:
                        nc.tensor.transpose(x_t[:, j - first, jn, :], block, ident_bf[:])
                    else:
                        nc.tensor.matmul(
                            x_t[:, j - first, jn, :], lhsT=block, rhs=ident_bf[:],
                            start=True, stop=True,
                        )
            x_banks[g, t, first] = x_t[:].rearrange("p j jn m -> p j m jn")

        def copy_x(g, t, first, last, engine="scalar"):
            if (g, t) not in x_by_n_tiles:
                x_by_n = x_stage.tile([P, PACK, P, PACK], BF16, name="x_by_n", align_bytes=64)
                x_by_n_tiles[g, t] = x_by_n
            dst = x_by_n_tiles[g, t][:, first:last]
            src = x_banks[g, t, first]
            if engine == "scalar":
                nc.scalar.copy(out=dst, in_=src)
            else:
                nc.vector.tensor_copy(out=dst, in_=src)

        def quantise_nodes(g, t):
            nc.vector.quantize_mx(
                out=xn_words[:, t, g, :].bitcast(FP8X4),
                scales=xn_plane[:, t, g, :],
                in_=x_by_n_tiles[g, t][:].rearrange("p j m jn -> p (j m jn)"),
            )

        xc_words = keep.tile([P, TIMES, NODES], U32, align_bytes=64)
        xc_plane = keep.tile([P, TIMES, NODES], U8, align_bytes=64)

        def quantise_channels(t, i, count=1):
            nodes = slice(i * PIECE_NODES, (i + count) * PIECE_NODES)
            nc.vector.quantize_mx(
                out=xc_words[:, t, nodes].bitcast(FP8X4),
                scales=xc_plane[:, t, nodes],
                in_=x_by_c[:, t, nodes, :].rearrange("p n j -> p (n j)"),
            )

        s_words = keep.tile([P, CHUNKS, PASSES * P], U32, align_bytes=64)
        s_plane = keep.tile([P, CHUNKS, PASSES * P], U8, align_bytes=64)
        r_rows = []
        s_tiles = []
        for v in range(CHUNKS):
            s_by_n = s_stage.tile([P, PASSES, P, PACK], BF16, name="s_by_n", align_bytes=64)
            s_tiles.append(s_by_n)
        tx_tiles = {}

        def scale_columns(v):
            cols = slice(v * P, (v + 1) * P)
            s_by_n = s_tiles[v]
            row = r_rows[v // PACK][:, (v % PACK) * P : (v % PACK + 1) * P]
            for g in range(PASSES) if v < PACK else (1,):
                nc.vector.tensor_tensor(
                    out=s_by_n[:, g].rearrange("p (b i) jn -> p b jn i", i=4),
                    in0=a2[:, g * PACK : (g + 1) * PACK, cols].rearrange("p jn (b i) -> p b jn i", i=4),
                    in1=row.rearrange("p (b i) -> p b i", i=4)
                    .unsqueeze(2)
                    .to_broadcast([P, P // 4, PACK, 4]),
                    op=ALU.mult,
                )

        def mirror(v, engine="scalar"):
            s_t = banks.tile([P, PACK, P], BF16, name="bank")
            for jn in range(PACK):
                nc.tensor.matmul(
                    s_t[:, jn, :], lhsT=s_tiles[jn][:, 1, :, v - PACK], rhs=ident_bf[:],
                    start=True, stop=True,
                )
            dst, src = s_tiles[v][:, 0], s_t[:].rearrange("p jn q -> p q jn")
            if engine == "scalar":
                nc.scalar.copy(out=dst, in_=src)
            else:
                nc.vector.tensor_copy(out=dst, in_=src)

        def quantise_columns(v):
            nc.vector.quantize_mx(
                out=s_words[:, v, :].bitcast(FP8X4),
                scales=s_plane[:, v, :],
                in_=s_tiles[v][:].rearrange("p g q jn -> p (g q jn)"),
            )

        def node_matmul(v, t, engine="scalar"):
            if t == 0:
                tx_by_c = stage.tile([P, TIMES, P * PACK], BF16, name="tx_by_c", align_bytes=64)
                tx_tiles[v] = tx_by_c
            tx_by_c = tx_tiles[v]
            tx = banks.tile([P, BANK], F32, name="bank")
            for j in range(PACK):
                for g in range(PASSES):
                    nc.tensor.matmul_mx(
                        out=tx[:, j * P : (j + 1) * P],
                        lhsT=xn_words[:, t, g, j * P : (j + 1) * P].bitcast(FP8X4),
                        lhsT_scale=xn_plane[:, t, g, j * P : (j + 1) * P],
                        rhs=s_words[:, v, g * P : (g + 1) * P].bitcast(FP8X4),
                        rhs_scale=s_plane[:, v, g * P : (g + 1) * P],
                        start=(g == 0),
                        stop=(g == PASSES - 1),
                    )
            dst = tx_by_c[:, t, :].rearrange("p (q j) -> p q j", j=PACK)
            src = tx[:].rearrange("p (j q) -> p q j", j=PACK)
            if engine == "scalar":
                nc.scalar.copy(out=dst, in_=src)
            else:
                nc.vector.tensor_copy(out=dst, in_=src)

        def quantise_tx(v):
            tx_by_c = tx_tiles[v]
            tx_words = stage.tile([P, TIMES, P], U32, name="tx_words", align_bytes=64)
            tx_plane = stage.tile([P, TIMES, P], U8, name="tx_plane", align_bytes=64)
            for times in (slice(0, 2), slice(2, 3)):
                nc.vector.quantize_mx(
                    out=tx_words[:, times, :].rearrange("p t q -> p (t q)").bitcast(FP8X4),
                    scales=tx_plane[:, times, :].rearrange("p t q -> p (t q)"),
                    in_=tx_by_c[:, times, :].rearrange("p t q -> p (t q)"),
                )
            tx_tiles[v] = (tx_words, tx_plane)

        def channel_matmuls(v, parts=((0, TIMES, "scalar"),), pool=out_banks, tag="acc"):
            tx_words, tx_plane = tx_tiles[v]
            acc = pool.tile([P, TIMES, OUTS], F32, name=tag)
            for t in range(TIMES):
                nc.tensor.matmul_mx(
                    out=acc[:, t, :],
                    lhsT=xc_words[:, t, v * P : (v + 1) * P].bitcast(FP8X4),
                    lhsT_scale=xc_plane[:, t, v * P : (v + 1) * P],
                    rhs=weights[0][0][:].bitcast(FP8X4),
                    rhs_scale=weights[0][1][:],
                    start=True,
                    stop=False,
                )
                nc.tensor.matmul_mx(
                    out=acc[:, t, :],
                    lhsT=tx_words[:, t, :].bitcast(FP8X4),
                    lhsT_scale=tx_plane[:, t, :],
                    rhs=weights[1][0][:].bitcast(FP8X4),
                    rhs_scale=weights[1][1][:],
                    start=False,
                    stop=True,
                )
            result = stage.tile([P, TIMES, OUTS], F32, name="result")
            for first, last, engine in parts:
                if engine == "scalar":
                    nc.scalar.copy(out=result[:, first:last], in_=acc[:, first:last])
                else:
                    nc.vector.tensor_copy(out=result[:, first:last], in_=acc[:, first:last])
                nc.sync.dma_start(
                    out=out[0, first:last, v * P : (v + 1) * P, :].rearrange("t q o -> q t o"),
                    in_=result[:, first:last],
                )

        for j in range(2):
            for t in range(TIMES):
                if t == 1:
                    turn_x(0, t, j, j + 1, banks, "bank")
                else:
                    turn_x(0, t, j, j + 1)
                copy_x(0, t, j, j + 1, "vector")
        for r in range(PACK):
            add_transposed(r, 0, PACK, 0)
        for i, t in ((0, 1), (1, 1), (0, 2), (1, 2), (2, 0), (3, 0)):
            group_channels(i, t, "gpsimd")
        add_transposed(4, 0, PACK, 0)
        group_channels(0, 0, "vector")
        add_transposed(5, 0, PACK, 0)
        turn_x(0, 0, 2, 4)
        copy_x(0, 0, 2, 4)
        add_transposed(6, 0, PACK, 0)
        sum_transposed(0, row_banks, "r_row0")
        sum_rest(0)
        add_transposed(7, 0, PACK, 0)
        sum_transposed(1, row_banks, "r_row1")
        sum_rest(1)
        nc.scalar.activation(out=warm[:], in_=warm[:], func=ACT.Sqrt)
        add_transposed(4, PACK, PACK, 1)
        add_transposed(5, PACK, PACK, 1)
        sum_transposed(2, row_banks, "r_row0")
        add_transposed(6, PACK, PACK, 1)
        sum_transposed(3, row_banks, "r_row1")
        add_transposed(7, PACK, PACK, 1)
        sum_rest(2)
        sum_rest(3)
        turn_x(1, 0, 0, 2)
        turn_x(1, 0, 2, 4)
        turn_x(0, 1, 2, 4, pool=banks, tag="bank")

        deg = keep.tile([P, CHUNKS], F32)
        nc.vector.tensor_reduce(out=deg[:], in_=deg_parts[:], axis=AXIS.X, op=ALU.add)
        rest = keep.tile([P, PACK], F32)
        nc.vector.tensor_reduce(out=rest[:], in_=row_rest[:], axis=AXIS.X, op=ALU.add)
        nc.vector.tensor_tensor(out=deg[:, :PACK], in0=deg[:, :PACK], in1=rest[:], op=ALU.add)
        root = keep.tile([P, CHUNKS], F32)
        nc.scalar.activation(out=root[:], in_=deg[:], func=ACT.Sqrt)
        r_col = keep.tile([P, CHUNKS], F32)
        nc.vector.reciprocal(out=r_col[:], in_=root[:])
        for h in range(HALVES):
            r_row = row_banks.tile([P, BANK], F32, name="r_row%d" % h)
            for i in range(BANK // P):
                r = h * (BANK // P) + i
                nc.tensor.transpose(
                    r_row[:, i * P : (i + 1) * P], r_col[:, r : r + 1].to_broadcast([P, P]), ident[:]
                )
            r_rows.append(r_row)
        copy_x(1, 0, 0, 2)
        copy_x(1, 0, 2, 4)
        copy_x(0, 1, 2, 4)
        turn_x(1, 1, 0, 2)
        turn_x(1, 1, 2, 4)
        copy_x(1, 1, 0, 2)
        copy_x(1, 1, 2, 4)
        scale_rows(range(CHUNKS), 0, 2 * P)
        scale_columns(0)
        quantise_nodes(0, 0)
        quantise_columns(0)
        quantise_nodes(1, 0)
        node_matmul(0, 0)
        scale_columns(1)
        quantise_nodes(0, 1)
        quantise_columns(1)
        turn_x(0, 2, 2, 4)
        turn_x(1, 2, 0, 2)
        copy_x(0, 2, 2, 4)
        copy_x(1, 2, 0, 2)
        node_matmul(1, 0)
        quantise_nodes(1, 1)
        node_matmul(0, 1)
        turn_x(1, 2, 2, 4)
        copy_x(1, 2, 2, 4)
        node_matmul(1, 1)
        scale_rows(range(CHUNKS), 2 * P, 2 * P)
        scale_columns(2)
        quantise_channels(0, 0, 2)
        quantise_columns(2)
        node_matmul(2, 0)
        node_matmul(2, 1)
        quantise_nodes(0, 2)
        quantise_nodes(1, 2)
        scale_columns(3)
        quantise_channels(1, 0, 2)
        quantise_columns(3)
        for v in range(3):
            node_matmul(v, 2)
        scale_rows(range(PACK, CHUNKS), BANK, BANK)
        mirror(4)
        mirror(5)
        quantise_channels(2, 0, 2)
        quantise_tx(0)
        scale_columns(4)
        quantise_tx(1)
        quantise_columns(4)

        for v in range(3, CHUNKS):
            for t in range(TIMES):
                node_matmul(v, t)
            if v == 3:
                mirror(6)
                mirror(7)
            channel_matmuls(v - 3)
            if v < 5:
                scale_columns(v + 2)
            if v == 4:
                scale_columns(7)
            quantise_tx(v - 1)
            if v < 5:
                quantise_columns(v + 2)
            if v == 4:
                quantise_columns(7)
            if v == 5:
                group_channels(2, 1, "vector")
                quantise_channels(0, 2, 2)
                group_channels(2, 2, "vector")
                quantise_channels(1, 2, 2)
                quantise_channels(2, 2, 2)
        channel_matmuls(CHUNKS - 3, ((0, TIMES, "scalar"),), banks, "bank")
        quantise_tx(CHUNKS - 1)
        channel_matmuls(CHUNKS - 2, ((0, TIMES, "scalar"),), banks, "bank")
        channel_matmuls(CHUNKS - 1, ((0, 2, "scalar"), (2, TIMES, "vector")), banks, "bank")
